import numpy as np
import ml_dtypes


def mxq(x, axis, fmt="e4m3"):
    dtype, down = {"e4m3": (ml_dtypes.float8_e4m3fn, 7), "e5m2": (ml_dtypes.float8_e5m2, 14)}[fmt]
    v = np.moveaxis(np.asarray(x, np.float32).astype(ml_dtypes.bfloat16).astype(np.float64), axis, -1)
    blocks = v.reshape(v.shape[:-1] + (-1, 32))
    amax = np.abs(blocks).max(-1, keepdims=True)
    byte = np.maximum(np.where(amax > 0, np.frexp(amax)[1] - 1 + 127, 0) - down, 1)
    scale = np.exp2(byte - 127.0)
    codes = (blocks / scale).astype(np.float32).astype(dtype).astype(np.float64)
    return np.moveaxis((codes * scale).reshape(v.shape), -1, axis)


WIDE = False


def mx_kscale(k):
    if not WIDE:
        return np.ones(k)
    levels = np.array([10, -10, 5, -5, 0])
    a = np.random.permutation(np.resize(levels, k // 512 * 4)).reshape(k // 512, 4)
    idx = np.arange(k)
    return np.exp2(a[idx // 512, idx % 128 // 32])


BF16 = ml_dtypes.bfloat16


def bf(x):
    return np.asarray(x, np.float32).astype(BF16)


def f64(x):
    return np.asarray(x).astype(np.float64)


E2M1 = np.array([0.0, 0.5, 1.0, 1.5, 2.0, 3.0, 4.0, 6.0, -0.0, -0.5, -1.0, -1.5, -2.0, -3.0, -4.0, -6.0])


def pack_weight(w, fmt):
    k, n = w.shape
    w = f64(bf(w)).reshape(k // 32, 32, n)
    amax = np.abs(w).max(1)
    if fmt == "e4m3":
        byte = np.frexp(amax)[1] - 1 + 127 - 7
    else:
        mant, ex = np.frexp(amax / 6.0)
        byte = np.where(mant > 0.5, ex, ex - 1) + 127
    byte = np.clip(np.where(amax > 0, byte, 1), 1, 254)
    scaled = (w * np.exp2(127.0 - byte)[:, None, :]).reshape(k, n).astype(np.float32)
    by_word = np.ascontiguousarray(scaled.reshape(k // 512, 128, 4, n).transpose(0, 1, 3, 2))
    if fmt == "e4m3":
        words = by_word.astype(ml_dtypes.float8_e4m3fn).view(np.uint8)
    else:
        c = by_word.astype(ml_dtypes.float4_e2m1fn).view(np.uint8) & 0xF
        words = c[..., 0::2] | (c[..., 1::2] << 4)
    return np.ascontiguousarray(words), np.ascontiguousarray(byte.astype(np.uint8).reshape(k // 512, 16, n))


def unpack_weight(words, scales, fmt):
    g, p, n, _ = words.shape
    if fmt == "e4m3":
        vals = np.ascontiguousarray(words).view(ml_dtypes.float8_e4m3fn).astype(np.float64)
    else:
        nib = np.empty((g, p, n, 4), np.uint8)
        nib[..., 0::2] = words & 0xF
        nib[..., 1::2] = words >> 4
        vals = E2M1[nib]
    vals = vals * np.repeat(np.exp2(scales.astype(np.float64) - 127.0), 8, axis=1)[..., None]
    return vals.transpose(0, 1, 3, 2).reshape(g * 512, n)


B, D, T = 2, 512, 2048


def setup_inputs():
    s = mx_kscale(D)
    t = s / s.max()
    y = (np.random.standard_normal((B, D, T)) * 2.0 + np.random.standard_normal((B, D, 1)) * 0.7) * t[:, None]
    u = np.random.standard_normal((B, D, T))
    z = np.random.standard_normal((B, D, T))
    words, scales = pack_weight(np.random.standard_normal((D, D)) * 0.3 * np.sqrt(D) / t[:, None], "e4m3")
    return {"x": bf(np.concatenate((y, u, z), axis=1)),
            "W_words": words,
            "W_scales": scales}


def reference(x, W_words, W_scales):
    x = f64(x)
    W = unpack_weight(W_words, W_scales, "e4m3")
    d = W.shape[0]
    y = np.swapaxes(x[:, :d, :], 1, 2)
    w = np.swapaxes(x[:, d:2 * d, :], 1, 2)
    intensity = np.exp(x[:, d:2 * d, :])
    e = np.exp(w - w.max(-1, keepdims=True))
    sm = e / e.sum(-1, keepdims=True)
    mean = y.mean(axis=1, keepdims=True)
    a = sm * (y - mean)
    rep = (mxq(a, 2, "e4m3") @ W) + mean
    rep1 = np.swapaxes(rep, 1, 2)
    y_trans = x[:, 2 * d:3 * d, :] - rep1
    return np.concatenate((rep1, intensity, y_trans), axis=1)

@@ -1,0 +1,260 @@
+from contextlib import ExitStack
+
+import concourse.mybir as mybir
+from concourse.masks import make_identity
+
+F32 = mybir.dt.float32
+BF16 = mybir.dt.bfloat16
+I32 = mybir.dt.int32
+U32 = mybir.dt.uint32
+U8 = mybir.dt.uint8
+FP8X4 = mybir.dt.float8_e4m3fn_x4
+ALU = mybir.AluOpType
+ACT = mybir.ActivationFunctionType
+AXIS = mybir.AxisListType
+
+B = 2
+D = 512
+T = 2048
+P = 128
+PACK = 4
+G = D // P
+TB = P
+CH = 512
+KB = CH // TB
+NCH = T // CH
+NC = B * NCH
+
+FLOPS = 2 * B * T * D * D
+
+
+def tile_crosschannelinterp_kernel(tc, x, W_words, W_scales, out):
+    nc = tc.nc
+    with ExitStack() as ctx:
+        const = ctx.enter_context(tc.tile_pool(name="const", bufs=1))
+        inputs = ctx.enter_context(tc.tile_pool(name="inputs", bufs=1))
+        work = ctx.enter_context(tc.tile_pool(name="work", bufs=2))
+        psum = ctx.enter_context(tc.psum_pool(name="psum", bufs=2))
+
+        y_dram = [x[b, 0:D, :].rearrange("(p j) t -> p j t", j=PACK) for b in range(B)]
+        u_dram = [x[b, D : 2 * D, :].rearrange("(p j) t -> p j t", j=PACK) for b in range(B)]
+        z_dram = [x[b, 2 * D : 3 * D, :].rearrange("(g m) t -> m g t", m=P) for b in range(B)]
+        rep_dram = [out[b, 0:D, :].rearrange("(g m) t -> m g t", m=P) for b in range(B)]
+        grown_dram = [out[b, D : 2 * D, :].rearrange("(p j) t -> p j t", j=PACK) for b in range(B)]
+        rest_dram = [out[b, 2 * D : 3 * D, :].rearrange("(g m) t -> m g t", m=P) for b in range(B)]
+
+        y_sb = [inputs.tile([P, PACK, T], BF16, name="y%d" % b) for b in range(B)]
+        u_sb = [inputs.tile([P, PACK, T], BF16, name="u%d" % b) for b in range(B)]
+        z_sb = [inputs.tile([P, G, T], BF16, name="z%d" % b) for b in range(B)]
+        w_codes = const.tile([P, PACK * D], U8, align_bytes=64)
+        w_scales = const.tile([P, D], U8, align_bytes=64)
+
+        nc.vector.memset(w_scales[:].bitcast(I32), 0)
+        for j in range(PACK):
+            nc.sync.dma_start(out=u_sb[0][:, j, :], in_=u_dram[0][:, j, :])
+        for j in range(PACK):
+            nc.sync.dma_start(out=y_sb[0][:, j, :], in_=y_dram[0][:, j, :])
+        nc.sync.dma_start(
+            out=w_codes[:].bitcast(I32),
+            in_=W_words[0].rearrange("p n t -> p (n t)").bitcast(I32),
+        )
+        for q in range(4):
+            nc.sync.dma_start(
+                out=w_scales[32 * q : 32 * q + 4, :].bitcast(I32),
+                in_=W_scales[0, 4 * q : 4 * q + 4, :].bitcast(I32),
+            )
+        nc.sync.dma_start(out=u_sb[1][:], in_=u_dram[1])
+        nc.sync.dma_start(out=z_sb[0][:], in_=z_dram[0])
+        nc.sync.dma_start(out=y_sb[1][:], in_=y_dram[1])
+        nc.sync.dma_start(out=z_sb[1][:], in_=z_dram[1])
+
+        ident_bf = const.tile([P, P], BF16)
+        make_identity(nc, ident_bf[:])
+        ident_f32 = const.tile([P, P], F32)
+        make_identity(nc, ident_f32[:])
+        lane_mask = const.tile([P, 32], F32)
+        nc.vector.tensor_reduce(
+            out=lane_mask[:], in_=ident_f32[:].rearrange("p (q r) -> p r q", q=4), axis=AXIS.X, op=ALU.add
+        )
+        quad_mask = const.tile([P, G], F32)
+        nc.vector.tensor_reduce(
+            out=quad_mask[:], in_=ident_f32[:].rearrange("p (g r) -> p g r", g=G), axis=AXIS.X, op=ALU.add
+        )
+
+        y_sum = const.tile([P, B, PACK], F32)
+        mean_by_lane = const.tile([P, B, PACK], F32)
+        mean_by_block = const.tile([P, B, G], F32)
+        top = const.tile([P, B, T // TB], F32)
+        neg_top = const.tile([P, B, T // TB], F32)
+        e_sum = const.tile([P, NC, KB], F32)
+        e_inv = const.tile([P, NC, KB], F32)
+        scrap = const.tile([P, T], BF16)
+
+        def time_mean(b):
+            for j in range(PACK):
+                nc.vector.tensor_scalar(
+                    out=scrap[:],
+                    in0=y_sb[b][:, j, :],
+                    scalar1=1.0,
+                    scalar2=None,
+                    op0=ALU.mult,
+                    op1=ALU.add,
+                    accum_out=y_sum[:, b, j : j + 1],
+                )
+            nc.vector.tensor_scalar(
+                out=mean_by_lane[:, b, :], in0=y_sum[:, b, :], scalar1=1.0 / T, scalar2=None, op0=ALU.mult
+            )
+            spread = work.tile([P, 32, PACK], F32, tag="spread")
+            nc.vector.tensor_tensor(
+                out=spread[:],
+                in0=lane_mask[:].unsqueeze(2).to_broadcast([P, 32, PACK]),
+                in1=mean_by_lane[:, b, :].unsqueeze(1).to_broadcast([P, 32, PACK]),
+                op=ALU.mult,
+            )
+            moved = psum.tile([P, CH], F32, tag="acc", bufs=3)
+            nc.tensor.matmul(
+                out=moved[:, 0:G],
+                lhsT=spread[:].rearrange("p r j -> p (r j)"),
+                rhs=quad_mask[:],
+                start=True,
+                stop=True,
+            )
+            nc.vector.tensor_copy(out=mean_by_block[:, b, :], in_=moved[:, 0:G])
+
+        def channel_max(b):
+            pair_max = work.tile([P, 2, T], BF16, tag="pair_max", bufs=1)
+            nc.vector.tensor_tensor(
+                out=pair_max[:], in0=u_sb[b][:, 0:2, :], in1=u_sb[b][:, 2:4, :], op=ALU.max
+            )
+            lane_max = work.tile([P, T], BF16, tag="lane_max", bufs=1)
+            nc.vector.tensor_tensor(
+                out=lane_max[:], in0=pair_max[:, 0, :], in1=pair_max[:, 1, :], op=ALU.max
+            )
+            for half in range(2):
+                flipped = psum.tile([P, 8, TB], BF16, tag="flip", bufs=2)
+                for k in range(8):
+                    tb = 8 * half + k
+                    nc.tensor.transpose(flipped[:, k, :], lane_max[:, tb * TB : (tb + 1) * TB], ident_bf[:])
+                nc.vector.tensor_reduce(
+                    out=top[:, b, 8 * half : 8 * half + 8], in_=flipped[:], axis=AXIS.X, op=ALU.max
+                )
+            nc.vector.tensor_scalar(
+                out=neg_top[:, b, :], in0=top[:, b, :], scalar1=-1.0, scalar2=None, op0=ALU.mult
+            )
+
+        def softmax_by_time(c):
+            b, ch = divmod(c, NCH)
+            sm_t = work.tile([P, KB, D], F32, tag="sm_t")
+            for half in range(KB // 2):
+                flipped = psum.tile([P, 2, D], BF16, tag="flip", bufs=2)
+                for h in range(2):
+                    tb = KB * ch + 2 * half + h
+                    for j in range(PACK):
+                        nc.tensor.transpose(
+                            flipped[:, h, j * P : (j + 1) * P],
+                            u_sb[b][:, j, tb * TB : (tb + 1) * TB],
+                            ident_bf[:],
+                        )
+                for h in range(2):
+                    k = 2 * half + h
+                    tb = KB * ch + k
+                    nc.scalar.activation(
+                        out=sm_t[:, k, :],
+                        in_=flipped[:, h, :],
+                        func=ACT.Exp,
+                        bias=neg_top[:, b, tb : tb + 1],
+                        scale=1.0,
+                        accum_out=e_sum[:, c, k : k + 1],
+                    )
+            nc.vector.reciprocal(out=e_inv[:, c, :], in_=e_sum[:, c, :])
+            for k in range(KB):
+                nc.vector.tensor_scalar(
+                    out=sm_t[:, k, :],
+                    in0=sm_t[:, k, :],
+                    scalar1=e_inv[:, c, k : k + 1],
+                    scalar2=None,
+                    op0=ALU.mult,
+                )
+            return sm_t
+
+        def quantised_a(c, sm_t):
+            b, ch = divmod(c, NCH)
+            cols = slice(ch * CH, (ch + 1) * CH)
+            a_rows = work.tile([P, PACK, CH], BF16, tag="a_rows")
+            for j in range(PACK):
+                sm = psum.tile([P, CH], F32, tag="sm", bufs=3)
+                for k in range(KB):
+                    nc.tensor.transpose(
+                        sm[:, k * TB : (k + 1) * TB], sm_t[:, k, j * P : (j + 1) * P], ident_f32[:]
+                    )
+                nc.vector.scalar_tensor_tensor(
+                    out=a_rows[:, j, :],
+                    in0=y_sb[b][:, j, cols],
+                    scalar=mean_by_lane[:, b, j : j + 1],
+                    in1=sm[:],
+                    op0=ALU.subtract,
+                    op1=ALU.mult,
+                )
+            a_grouped = work.tile([P, CH, PACK], BF16, tag="a_grouped", align_bytes=64)
+            nc.vector.tensor_copy(
+                out=a_grouped[:].rearrange("p (c i) j -> p c j i", i=4),
+                in_=a_rows[:].rearrange("p j (c i) -> p c j i", i=4),
+            )
+            a_codes = work.tile([P, CH], U32, tag="a_codes", align_bytes=64)
+            a_scales = work.tile([P, CH], U8, tag="a_scales", align_bytes=64)
+            nc.vector.quantize_mx(
+                out=a_codes[:].bitcast(FP8X4),
+                scales=a_scales[:],
+                in_=a_grouped[:].rearrange("p t j -> p (t j)"),
+            )
+            return a_codes, a_scales
+
+        def mix_and_store(c, a_codes, a_scales):
+            b, ch = divmod(c, NCH)
+            cols = slice(ch * CH, (ch + 1) * CH)
+            rep_sb = work.tile([P, G, CH], F32, tag="rep_sb")
+            rest_sb = work.tile([P, G, CH], F32, tag="rest_sb")
+            for g in range(G):
+                acc = psum.tile([P, CH], F32, tag="acc", bufs=3)
+                nc.tensor.matmul_mx(
+                    out=acc[:],
+                    lhsT=w_codes[:, g * PACK * P : (g + 1) * PACK * P].bitcast(FP8X4),
+                    lhsT_scale=w_scales[:, g * P : (g + 1) * P],
+                    rhs=a_codes[:].bitcast(FP8X4),
+                    rhs_scale=a_scales[:],
+                    start=True,
+                    stop=True,
+                )
+                nc.scalar.activation(
+                    out=rep_sb[:, g, :],
+                    in_=acc[:],
+                    func=ACT.Identity,
+                    bias=mean_by_block[:, b, g : g + 1],
+                    scale=1.0,
+                )
+                nc.gpsimd.tensor_tensor(
+                    out=rest_sb[:, g, :], in0=z_sb[b][:, g, cols], in1=rep_sb[:, g, :], op=ALU.subtract
+                )
+            nc.sync.dma_start(out=rep_dram[b][:, :, cols], in_=rep_sb[:])
+            nc.sync.dma_start(out=rest_dram[b][:, :, cols], in_=rest_sb[:])
+
+        def intensity(b, j):
+            grown = work.tile([P, T], F32, tag="grown", bufs=3)
+            nc.scalar.activation(out=grown[:], in_=u_sb[b][:, j, :], func=ACT.Exp)
+            nc.sync.dma_start(out=grown_dram[b][:, j, :], in_=grown[:])
+
+        softmaxes = {}
+        operands = {}
+        channel_max(0)
+        time_mean(0)
+        for i in range(NC + 2):
+            if i < NC:
+                softmaxes[i] = softmax_by_time(i)
+                intensity(i // PACK, i % PACK)
+            if i == 1:
+                channel_max(1)
+                time_mean(1)
+            if 1 <= i <= NC:
+                operands[i - 1] = quantised_a(i - 1, softmaxes[i - 1])
+            if i >= 2:
+                mix_and_store(i - 2, operands[i - 2][0], operands[i - 2][1])

@@ -24,6 +24,7 @@ CH = 512
 KB = CH // TB
 NCH = T // CH
 NC = B * NCH
+AHEAD = 3
 
 FLOPS = 2 * B * T * D * D
 
@@ -49,6 +50,8 @@ def tile_crosschannelinterp_kernel(tc, x, W_words, W_scales, out):
         w_codes = const.tile([P, PACK * D], U8, align_bytes=64)
         w_scales = const.tile([P, D], U8, align_bytes=64)
 
+        ctx.enter_context(tc.manual_schedule())
+
         nc.vector.memset(w_scales[:].bitcast(I32), 0)
         for j in range(PACK):
             nc.sync.dma_start(out=u_sb[0][:, j, :], in_=u_dram[0][:, j, :])
@@ -63,10 +66,6 @@ def tile_crosschannelinterp_kernel(tc, x, W_words, W_scales, out):
                 out=w_scales[32 * q : 32 * q + 4, :].bitcast(I32),
                 in_=W_scales[0, 4 * q : 4 * q + 4, :].bitcast(I32),
             )
-        nc.sync.dma_start(out=u_sb[1][:], in_=u_dram[1])
-        nc.sync.dma_start(out=z_sb[0][:], in_=z_dram[0])
-        nc.sync.dma_start(out=y_sb[1][:], in_=y_dram[1])
-        nc.sync.dma_start(out=z_sb[1][:], in_=z_dram[1])
 
         ident_bf = const.tile([P, P], BF16)
         make_identity(nc, ident_bf[:])
@@ -88,9 +87,9 @@ def tile_crosschannelinterp_kernel(tc, x, W_words, W_scales, out):
         neg_top = const.tile([P, B, T // TB], F32)
         e_sum = const.tile([P, NC, KB], F32)
         e_inv = const.tile([P, NC, KB], F32)
-        scrap = const.tile([P, T], BF16)
 
         def time_mean(b):
+            scrap = work.tile([P, T], BF16, tag="pair_a", bufs=1)
             for j in range(PACK):
                 nc.vector.tensor_scalar(
                     out=scrap[:],
@@ -121,15 +120,16 @@ def tile_crosschannelinterp_kernel(tc, x, W_words, W_scales, out):
             )
             nc.vector.tensor_copy(out=mean_by_block[:, b, :], in_=moved[:, 0:G])
 
-        def channel_max(b):
-            pair_max = work.tile([P, 2, T], BF16, tag="pair_max", bufs=1)
-            nc.vector.tensor_tensor(
-                out=pair_max[:], in0=u_sb[b][:, 0:2, :], in1=u_sb[b][:, 2:4, :], op=ALU.max
-            )
+        def fold_channels(b):
+            pair_a = work.tile([P, T], BF16, tag="pair_a", bufs=1)
+            nc.vector.tensor_tensor(out=pair_a[:], in0=u_sb[b][:, 0, :], in1=u_sb[b][:, 1, :], op=ALU.max)
+            pair_b = work.tile([P, T], BF16, tag="pair_b", bufs=1)
+            nc.vector.tensor_tensor(out=pair_b[:], in0=u_sb[b][:, 2, :], in1=u_sb[b][:, 3, :], op=ALU.max)
             lane_max = work.tile([P, T], BF16, tag="lane_max", bufs=1)
-            nc.vector.tensor_tensor(
-                out=lane_max[:], in0=pair_max[:, 0, :], in1=pair_max[:, 1, :], op=ALU.max
-            )
+            nc.vector.tensor_tensor(out=lane_max[:], in0=pair_a[:], in1=pair_b[:], op=ALU.max)
+            return lane_max
+
+        def top_of_time(b, lane_max):
             for half in range(2):
                 flipped = psum.tile([P, 8, TB], BF16, tag="flip", bufs=2)
                 for k in range(8):
@@ -142,9 +142,9 @@ def tile_crosschannelinterp_kernel(tc, x, W_words, W_scales, out):
                 out=neg_top[:, b, :], in0=top[:, b, :], scalar1=-1.0, scalar2=None, op0=ALU.mult
             )
 
-        def softmax_by_time(c):
+        def flip(c):
             b, ch = divmod(c, NCH)
-            sm_t = work.tile([P, KB, D], F32, tag="sm_t")
+            halves = []
             for half in range(KB // 2):
                 flipped = psum.tile([P, 2, D], BF16, tag="flip", bufs=2)
                 for h in range(2):
@@ -155,18 +155,28 @@ def tile_crosschannelinterp_kernel(tc, x, W_words, W_scales, out):
                             u_sb[b][:, j, tb * TB : (tb + 1) * TB],
                             ident_bf[:],
                         )
-                for h in range(2):
-                    k = 2 * half + h
-                    tb = KB * ch + k
-                    nc.scalar.activation(
-                        out=sm_t[:, k, :],
-                        in_=flipped[:, h, :],
-                        func=ACT.Exp,
-                        bias=neg_top[:, b, tb : tb + 1],
-                        scale=1.0,
-                        accum_out=e_sum[:, c, k : k + 1],
-                    )
+                halves.append(flipped)
+            return halves
+
+        def exponentials(c, halves):
+            b, ch = divmod(c, NCH)
+            sm_t = work.tile([P, KB, D], F32, tag="sm_t")
+            for k in range(KB):
+                tb = KB * ch + k
+                nc.scalar.activation(
+                    out=sm_t[:, k, :],
+                    in_=halves[k // 2][:, k % 2, :],
+                    func=ACT.Exp,
+                    bias=neg_top[:, b, tb : tb + 1],
+                    scale=1.0,
+                    accum_out=e_sum[:, c, k : k + 1],
+                )
+            return sm_t
+
+        def invert_sums(c):
             nc.vector.reciprocal(out=e_inv[:, c, :], in_=e_sum[:, c, :])
+
+        def normalise(c, sm_t):
             for k in range(KB):
                 nc.vector.tensor_scalar(
                     out=sm_t[:, k, :],
@@ -175,31 +185,33 @@ def tile_crosschannelinterp_kernel(tc, x, W_words, W_scales, out):
                     scalar2=None,
                     op0=ALU.mult,
                 )
-            return sm_t
 
-        def quantised_a(c, sm_t):
+        def back_flip(c, j, sm_t):
+            sm = psum.tile([P, CH], F32, tag="sm", bufs=AHEAD)
+            for k in range(KB):
+                nc.tensor.transpose(sm[:, k * TB : (k + 1) * TB], sm_t[:, k, j * P : (j + 1) * P], ident_f32[:])
+            return sm
+
+        def multiply(c, j, sm, a_rows):
             b, ch = divmod(c, NCH)
-            cols = slice(ch * CH, (ch + 1) * CH)
-            a_rows = work.tile([P, PACK, CH], BF16, tag="a_rows")
-            for j in range(PACK):
-                sm = psum.tile([P, CH], F32, tag="sm", bufs=3)
-                for k in range(KB):
-                    nc.tensor.transpose(
-                        sm[:, k * TB : (k + 1) * TB], sm_t[:, k, j * P : (j + 1) * P], ident_f32[:]
-                    )
-                nc.vector.scalar_tensor_tensor(
-                    out=a_rows[:, j, :],
-                    in0=y_sb[b][:, j, cols],
-                    scalar=mean_by_lane[:, b, j : j + 1],
-                    in1=sm[:],
-                    op0=ALU.subtract,
-                    op1=ALU.mult,
-                )
+            nc.vector.scalar_tensor_tensor(
+                out=a_rows[:, j, :],
+                in0=y_sb[b][:, j, ch * CH : (ch + 1) * CH],
+                scalar=mean_by_lane[:, b, j : j + 1],
+                in1=sm[:],
+                op0=ALU.subtract,
+                op1=ALU.mult,
+            )
+
+        def regroup(a_rows):
             a_grouped = work.tile([P, CH, PACK], BF16, tag="a_grouped", align_bytes=64)
             nc.vector.tensor_copy(
                 out=a_grouped[:].rearrange("p (c i) j -> p c j i", i=4),
                 in_=a_rows[:].rearrange("p j (c i) -> p c j i", i=4),
             )
+            return a_grouped
+
+        def quantise(a_grouped):
             a_codes = work.tile([P, CH], U32, tag="a_codes", align_bytes=64)
             a_scales = work.tile([P, CH], U8, tag="a_scales", align_bytes=64)
             nc.vector.quantize_mx(
@@ -212,8 +224,8 @@ def tile_crosschannelinterp_kernel(tc, x, W_words, W_scales, out):
         def mix_and_store(c, a_codes, a_scales):
             b, ch = divmod(c, NCH)
             cols = slice(ch * CH, (ch + 1) * CH)
-            rep_sb = work.tile([P, G, CH], F32, tag="rep_sb")
-            rest_sb = work.tile([P, G, CH], F32, tag="rest_sb")
+            rep_sb = work.tile([P, G, CH], F32, tag="rep_sb", bufs=3)
+            rest_sb = work.tile([P, G, CH], F32, tag="rest_sb", bufs=3)
             for g in range(G):
                 acc = psum.tile([P, CH], F32, tag="acc", bufs=3)
                 nc.tensor.matmul_mx(
@@ -239,22 +251,66 @@ def tile_crosschannelinterp_kernel(tc, x, W_words, W_scales, out):
             nc.sync.dma_start(out=rest_dram[b][:, :, cols], in_=rest_sb[:])
 
         def intensity(b, j):
-            grown = work.tile([P, T], F32, tag="grown", bufs=3)
+            grown = work.tile([P, T], F32, tag="grown", bufs=4)
             nc.scalar.activation(out=grown[:], in_=u_sb[b][:, j, :], func=ACT.Exp)
             nc.sync.dma_start(out=grown_dram[b][:, j, :], in_=grown[:])
 
+        intensity(0, 0)
+        intensity(0, 1)
+        nc.sync.dma_start(out=u_sb[1][:], in_=u_dram[1])
+        intensity(0, 2)
+        intensity(0, 3)
+        nc.sync.dma_start(out=z_sb[0][:], in_=z_dram[0])
+        top_of_time(0, fold_channels(0))
         softmaxes = {}
-        operands = {}
-        channel_max(0)
+        flips = {0: flip(0)}
+        softmaxes[0] = exponentials(0, flips[0])
+        flips[1] = flip(1)
+        softmaxes[1] = exponentials(1, flips[1])
         time_mean(0)
-        for i in range(NC + 2):
+        invert_sums(0)
+        normalise(0, softmaxes[0])
+        banks = {}
+        for j in range(AHEAD):
+            banks[(0, j)] = back_flip(0, j, softmaxes[0])
+        flips[2] = flip(2)
+
+        rows = {}
+        grouped = {}
+        folded = {}
+        for i in range(NC + 1):
+            if i + 1 < NC:
+                invert_sums(i + 1)
             if i < NC:
-                softmaxes[i] = softmax_by_time(i)
-                intensity(i // PACK, i % PACK)
+                rows[i] = work.tile([P, PACK, CH], BF16, tag="a_rows", name="a_rows")
+                multiply(i, 0, banks[(i, 0)], rows[i])
+                banks[(i, 3)] = back_flip(i, 3, softmaxes[i])
+                multiply(i, 1, banks[(i, 1)], rows[i])
+            if i >= 1:
+                a_codes, a_scales = quantise(grouped[i - 1])
+                mix_and_store(i - 1, a_codes, a_scales)
+            if i < NC:
+                multiply(i, 2, banks[(i, 2)], rows[i])
+                multiply(i, 3, banks[(i, 3)], rows[i])
+            if i + 1 < NC:
+                normalise(i + 1, softmaxes[i + 1])
+                for j in range(AHEAD):
+                    banks[(i + 1, j)] = back_flip(i + 1, j, softmaxes[i + 1])
+            if i < NC:
+                grouped[i] = regroup(rows[i])
+            if i + 2 < NC:
+                softmaxes[i + 2] = exponentials(i + 2, flips[i + 2])
+            if i == 0:
+                nc.sync.dma_start(out=y_sb[1][:], in_=y_dram[1])
             if i == 1:
-                channel_max(1)
+                nc.sync.dma_start(out=z_sb[1][:], in_=z_dram[1])
+            if i < PACK:
+                intensity(1, i)
+            if i == 0:
+                folded[1] = fold_channels(1)
+            if i == 1:
+                top_of_time(1, folded[1])
+            if i + 3 < NC:
+                flips[i + 3] = flip(i + 3)
+            if i == 2:
                 time_mean(1)
-            if 1 <= i <= NC:
-                operands[i - 1] = quantised_a(i - 1, softmaxes[i - 1])
-            if i >= 2:
-                mix_and_store(i - 2, operands[i - 2][0], operands[i - 2][1])

@@ -24,7 +24,8 @@ CH = 512
 KB = CH // TB
 NCH = T // CH
 NC = B * NCH
-AHEAD = 3
+HALF = T // 2
+AHEAD = 4
 
 FLOPS = 2 * B * T * D * D
 
@@ -53,10 +54,10 @@ def tile_crosschannelinterp_kernel(tc, x, W_words, W_scales, out):
         ctx.enter_context(tc.manual_schedule())
 
         nc.vector.memset(w_scales[:].bitcast(I32), 0)
-        for j in range(PACK):
-            nc.sync.dma_start(out=u_sb[0][:, j, :], in_=u_dram[0][:, j, :])
+        nc.sync.dma_start(out=u_sb[0][:, :, 0:HALF], in_=u_dram[0][:, :, 0:HALF])
         for j in range(PACK):
             nc.sync.dma_start(out=y_sb[0][:, j, :], in_=y_dram[0][:, j, :])
+        nc.sync.dma_start(out=u_sb[0][:, :, HALF:T], in_=u_dram[0][:, :, HALF:T])
         nc.sync.dma_start(
             out=w_codes[:].bitcast(I32),
             in_=W_words[0].rearrange("p n t -> p (n t)").bitcast(I32),
@@ -66,6 +67,10 @@ def tile_crosschannelinterp_kernel(tc, x, W_words, W_scales, out):
                 out=w_scales[32 * q : 32 * q + 4, :].bitcast(I32),
                 in_=W_scales[0, 4 * q : 4 * q + 4, :].bitcast(I32),
             )
+        nc.sync.dma_start(out=z_sb[0][:], in_=z_dram[0])
+        nc.sync.dma_start(out=u_sb[1][:], in_=u_dram[1])
+        nc.sync.dma_start(out=y_sb[1][:], in_=y_dram[1])
+        nc.sync.dma_start(out=z_sb[1][:], in_=z_dram[1])
 
         ident_bf = const.tile([P, P], BF16)
         make_identity(nc, ident_bf[:])
@@ -88,21 +93,24 @@ def tile_crosschannelinterp_kernel(tc, x, W_words, W_scales, out):
         e_sum = const.tile([P, NC, KB], F32)
         e_inv = const.tile([P, NC, KB], F32)
 
+        def time_sum(b, j):
+            scrap = work.tile([P, T], BF16, tag="scrap", bufs=1)
+            nc.vector.tensor_scalar(
+                out=scrap[:],
+                in0=y_sb[b][:, j, :],
+                scalar1=1.0,
+                scalar2=None,
+                op0=ALU.mult,
+                op1=ALU.add,
+                accum_out=y_sum[:, b, j : j + 1],
+            )
+
         def time_mean(b):
-            scrap = work.tile([P, T], BF16, tag="pair_a", bufs=1)
-            for j in range(PACK):
-                nc.vector.tensor_scalar(
-                    out=scrap[:],
-                    in0=y_sb[b][:, j, :],
-                    scalar1=1.0,
-                    scalar2=None,
-                    op0=ALU.mult,
-                    op1=ALU.add,
-                    accum_out=y_sum[:, b, j : j + 1],
-                )
             nc.vector.tensor_scalar(
                 out=mean_by_lane[:, b, :], in0=y_sum[:, b, :], scalar1=1.0 / T, scalar2=None, op0=ALU.mult
             )
+
+        def mean_to_blocks(b):
             spread = work.tile([P, 32, PACK], F32, tag="spread")
             nc.vector.tensor_tensor(
                 out=spread[:],
@@ -110,7 +118,7 @@ def tile_crosschannelinterp_kernel(tc, x, W_words, W_scales, out):
                 in1=mean_by_lane[:, b, :].unsqueeze(1).to_broadcast([P, 32, PACK]),
                 op=ALU.mult,
             )
-            moved = psum.tile([P, CH], F32, tag="acc", bufs=3)
+            moved = psum.tile([P, CH], F32, tag="acc", bufs=2)
             nc.tensor.matmul(
                 out=moved[:, 0:G],
                 lhsT=spread[:].rearrange("p r j -> p (r j)"),
@@ -118,28 +126,32 @@ def tile_crosschannelinterp_kernel(tc, x, W_words, W_scales, out):
                 start=True,
                 stop=True,
             )
+            return moved
+
+        def keep_block_means(b, moved):
             nc.vector.tensor_copy(out=mean_by_block[:, b, :], in_=moved[:, 0:G])
 
-        def fold_channels(b):
-            pair_a = work.tile([P, T], BF16, tag="pair_a", bufs=1)
-            nc.vector.tensor_tensor(out=pair_a[:], in0=u_sb[b][:, 0, :], in1=u_sb[b][:, 1, :], op=ALU.max)
-            pair_b = work.tile([P, T], BF16, tag="pair_b", bufs=1)
-            nc.vector.tensor_tensor(out=pair_b[:], in0=u_sb[b][:, 2, :], in1=u_sb[b][:, 3, :], op=ALU.max)
-            lane_max = work.tile([P, T], BF16, tag="lane_max", bufs=1)
+        def fold_lanes(b, half):
+            cols = slice(half * HALF, (half + 1) * HALF)
+            pair_a = work.tile([P, HALF], BF16, tag="pair_a", bufs=1)
+            nc.vector.tensor_tensor(out=pair_a[:], in0=u_sb[b][:, 0, cols], in1=u_sb[b][:, 1, cols], op=ALU.max)
+            pair_b = work.tile([P, HALF], BF16, tag="pair_b", bufs=1)
+            nc.vector.tensor_tensor(out=pair_b[:], in0=u_sb[b][:, 2, cols], in1=u_sb[b][:, 3, cols], op=ALU.max)
+            lane_max = work.tile([P, HALF], BF16, tag="lane_max", bufs=1)
             nc.vector.tensor_tensor(out=lane_max[:], in0=pair_a[:], in1=pair_b[:], op=ALU.max)
             return lane_max
 
-        def top_of_time(b, lane_max):
-            for half in range(2):
-                flipped = psum.tile([P, 8, TB], BF16, tag="flip", bufs=2)
-                for k in range(8):
-                    tb = 8 * half + k
-                    nc.tensor.transpose(flipped[:, k, :], lane_max[:, tb * TB : (tb + 1) * TB], ident_bf[:])
-                nc.vector.tensor_reduce(
-                    out=top[:, b, 8 * half : 8 * half + 8], in_=flipped[:], axis=AXIS.X, op=ALU.max
-                )
+        def flip_lane_max(lane_max):
+            flipped = psum.tile([P, 8, TB], BF16, tag="flip", bufs=2)
+            for k in range(8):
+                nc.tensor.transpose(flipped[:, k, :], lane_max[:, k * TB : (k + 1) * TB], ident_bf[:])
+            return flipped
+
+        def channel_max(b, half, flipped):
+            blocks = slice(8 * half, 8 * half + 8)
+            nc.vector.tensor_reduce(out=top[:, b, blocks], in_=flipped[:], axis=AXIS.X, op=ALU.max)
             nc.vector.tensor_scalar(
-                out=neg_top[:, b, :], in0=top[:, b, :], scalar1=-1.0, scalar2=None, op0=ALU.mult
+                out=neg_top[:, b, blocks], in0=top[:, b, blocks], scalar1=-1.0, scalar2=None, op0=ALU.mult
             )
 
         def flip(c):
@@ -160,7 +172,7 @@ def tile_crosschannelinterp_kernel(tc, x, W_words, W_scales, out):
 
         def exponentials(c, halves):
             b, ch = divmod(c, NCH)
-            sm_t = work.tile([P, KB, D], F32, tag="sm_t")
+            sm_t = work.tile([P, KB, D], F32, tag="sm_t", bufs=2)
             for k in range(KB):
                 tb = KB * ch + k
                 nc.scalar.activation(
@@ -221,96 +233,109 @@ def tile_crosschannelinterp_kernel(tc, x, W_words, W_scales, out):
             )
             return a_codes, a_scales
 
-        def mix_and_store(c, a_codes, a_scales):
+        def mix(g, a_codes, a_scales):
+            acc = psum.tile([P, CH], F32, tag="acc", bufs=2)
+            nc.tensor.matmul_mx(
+                out=acc[:],
+                lhsT=w_codes[:, g * PACK * P : (g + 1) * PACK * P].bitcast(FP8X4),
+                lhsT_scale=w_scales[:, g * P : (g + 1) * P],
+                rhs=a_codes[:].bitcast(FP8X4),
+                rhs_scale=a_scales[:],
+                start=True,
+                stop=True,
+            )
+            return acc
+
+        def finish(c, g, acc, rep_sb, rest_sb):
             b, ch = divmod(c, NCH)
             cols = slice(ch * CH, (ch + 1) * CH)
-            rep_sb = work.tile([P, G, CH], F32, tag="rep_sb", bufs=3)
-            rest_sb = work.tile([P, G, CH], F32, tag="rest_sb", bufs=3)
-            for g in range(G):
-                acc = psum.tile([P, CH], F32, tag="acc", bufs=3)
-                nc.tensor.matmul_mx(
-                    out=acc[:],
-                    lhsT=w_codes[:, g * PACK * P : (g + 1) * PACK * P].bitcast(FP8X4),
-                    lhsT_scale=w_scales[:, g * P : (g + 1) * P],
-                    rhs=a_codes[:].bitcast(FP8X4),
-                    rhs_scale=a_scales[:],
-                    start=True,
-                    stop=True,
-                )
-                nc.scalar.activation(
-                    out=rep_sb[:, g, :],
-                    in_=acc[:],
-                    func=ACT.Identity,
-                    bias=mean_by_block[:, b, g : g + 1],
-                    scale=1.0,
-                )
-                nc.gpsimd.tensor_tensor(
-                    out=rest_sb[:, g, :], in0=z_sb[b][:, g, cols], in1=rep_sb[:, g, :], op=ALU.subtract
-                )
-            nc.sync.dma_start(out=rep_dram[b][:, :, cols], in_=rep_sb[:])
-            nc.sync.dma_start(out=rest_dram[b][:, :, cols], in_=rest_sb[:])
+            nc.scalar.activation(
+                out=rep_sb[:, g, :], in_=acc[:], func=ACT.Identity, bias=mean_by_block[:, b, g : g + 1], scale=1.0
+            )
+            subtractor = nc.vector if c == NC - 1 else nc.gpsimd
+            subtractor.tensor_tensor(
+                out=rest_sb[:, g, :], in0=z_sb[b][:, g, cols], in1=rep_sb[:, g, :], op=ALU.subtract
+            )
+            if g % 2 == 1:
+                pair = slice(g - 1, g + 1)
+                nc.sync.dma_start(out=rep_dram[b][:, pair, cols], in_=rep_sb[:, pair, :])
+                nc.sync.dma_start(out=rest_dram[b][:, pair, cols], in_=rest_sb[:, pair, :])
 
         def intensity(b, j):
             grown = work.tile([P, T], F32, tag="grown", bufs=4)
             nc.scalar.activation(out=grown[:], in_=u_sb[b][:, j, :], func=ACT.Exp)
             nc.sync.dma_start(out=grown_dram[b][:, j, :], in_=grown[:])
 
-        intensity(0, 0)
-        intensity(0, 1)
-        nc.sync.dma_start(out=u_sb[1][:], in_=u_dram[1])
-        intensity(0, 2)
-        intensity(0, 3)
-        nc.sync.dma_start(out=z_sb[0][:], in_=z_dram[0])
-        top_of_time(0, fold_channels(0))
+        pieces = [(b, j) for b in range(B) for j in range(PACK)]
         softmaxes = {}
+        banks = {}
+        tops = {}
+        moved = {}
+        tops[(0, 0)] = flip_lane_max(fold_lanes(0, 0))
+        time_sum(0, 0)
+        channel_max(0, 0, tops[(0, 0)])
         flips = {0: flip(0)}
         softmaxes[0] = exponentials(0, flips[0])
-        flips[1] = flip(1)
-        softmaxes[1] = exponentials(1, flips[1])
+        for j in range(1, PACK):
+            time_sum(0, j)
         time_mean(0)
         invert_sums(0)
         normalise(0, softmaxes[0])
-        banks = {}
-        for j in range(AHEAD):
+        flips[1] = flip(1)
+        softmaxes[1] = exponentials(1, flips[1])
+        for j in range(PACK):
             banks[(0, j)] = back_flip(0, j, softmaxes[0])
-        flips[2] = flip(2)
+        tops[(0, 1)] = flip_lane_max(fold_lanes(0, 1))
+        moved[0] = mean_to_blocks(0)
+        intensity(0, 0)
+        intensity(0, 1)
 
-        rows = {}
-        grouped = {}
-        folded = {}
+        fold_at = {0: (1, 0), 2: (1, 1)}
+        reduce_at = {0: (0, 1), 1: (1, 0), 3: (1, 1)}
+        operands = {}
         for i in range(NC + 1):
-            if i + 1 < NC:
-                invert_sums(i + 1)
+            c = i - 1
             if i < NC:
-                rows[i] = work.tile([P, PACK, CH], BF16, tag="a_rows", name="a_rows")
-                multiply(i, 0, banks[(i, 0)], rows[i])
-                banks[(i, 3)] = back_flip(i, 3, softmaxes[i])
-                multiply(i, 1, banks[(i, 1)], rows[i])
+                a_rows = work.tile([P, PACK, CH], BF16, tag="a_rows")
+                for j in range(PACK):
+                    multiply(i, j, banks[(i, j)], a_rows)
+            if i in reduce_at:
+                channel_max(reduce_at[i][0], reduce_at[i][1], tops[reduce_at[i]])
+            if i % NCH == 0 and i < NC:
+                keep_block_means(i // NCH, moved[i // NCH])
             if i >= 1:
-                a_codes, a_scales = quantise(grouped[i - 1])
-                mix_and_store(i - 1, a_codes, a_scales)
-            if i < NC:
-                multiply(i, 2, banks[(i, 2)], rows[i])
-                multiply(i, 3, banks[(i, 3)], rows[i])
-            if i + 1 < NC:
-                normalise(i + 1, softmaxes[i + 1])
-                for j in range(AHEAD):
-                    banks[(i + 1, j)] = back_flip(i + 1, j, softmaxes[i + 1])
-            if i < NC:
-                grouped[i] = regroup(rows[i])
+                rep_sb = work.tile([P, G, CH], F32, tag="rep_sb", bufs=3)
+                rest_sb = work.tile([P, G, CH], F32, tag="rest_sb", bufs=3)
+                for g in (0, 1):
+                    finish(c, g, mix(g, operands[c][0], operands[c][1]), rep_sb, rest_sb)
+            if i + 2 < NC:
+                flips[i + 2] = flip(i + 2)
+            if i >= 1:
+                late_sums = [mix(g, operands[c][0], operands[c][1]) for g in (2, 3)]
             if i + 2 < NC:
                 softmaxes[i + 2] = exponentials(i + 2, flips[i + 2])
-            if i == 0:
-                nc.sync.dma_start(out=y_sb[1][:], in_=y_dram[1])
+            if i >= 1:
+                for g in (2, 3):
+                    finish(c, g, late_sums[g - 2], rep_sb, rest_sb)
+            if i < NC:
+                a_grouped = regroup(a_rows)
+            if i + 1 < NC:
+                invert_sums(i + 1)
+                normalise(i + 1, softmaxes[i + 1])
+            if i < NC:
+                operands[i] = quantise(a_grouped)
+            if i + 1 < NC:
+                for j in range(PACK):
+                    banks[(i + 1, j)] = back_flip(i + 1, j, softmaxes[i + 1])
+            for b, j in pieces[2 * i + 2 : 2 * i + 4]:
+                intensity(b, j)
+            if i in fold_at:
+                tops[fold_at[i]] = flip_lane_max(fold_lanes(fold_at[i][0], fold_at[i][1]))
             if i == 1:
-                nc.sync.dma_start(out=z_sb[1][:], in_=z_dram[1])
-            if i < PACK:
-                intensity(1, i)
-            if i == 0:
-                folded[1] = fold_channels(1)
-            if i == 1:
-                top_of_time(1, folded[1])
-            if i + 3 < NC:
-                flips[i + 3] = flip(i + 3)
-            if i == 2:
+                time_sum(1, 0)
+                time_sum(1, 1)
+            if i == 3:
+                time_sum(1, 2)
+                time_sum(1, 3)
                 time_mean(1)
+                moved[1] = mean_to_blocks(1)

@@ -88,7 +88,6 @@ def tile_crosschannelinterp_kernel(tc, x, W_words, W_scales, out):
         y_sum = const.tile([P, B, PACK], F32)
         mean_by_lane = const.tile([P, B, PACK], F32)
         mean_by_block = const.tile([P, B, G], F32)
-        top = const.tile([P, B, T // TB], F32)
         neg_top = const.tile([P, B, T // TB], F32)
         e_sum = const.tile([P, NC, KB], F32)
         e_inv = const.tile([P, NC, KB], F32)
@@ -143,46 +142,51 @@ def tile_crosschannelinterp_kernel(tc, x, W_words, W_scales, out):
 
         def flip_lane_max(lane_max):
             flipped = psum.tile([P, 8, TB], BF16, tag="flip", bufs=2)
-            for k in range(8):
-                nc.tensor.transpose(flipped[:, k, :], lane_max[:, k * TB : (k + 1) * TB], ident_bf[:])
+            for chunk in range(HALF // CH):
+                for e in range(2):
+                    for wb in range(2):
+                        first = chunk * CH + wb * 2 * P + e
+                        nc.tensor.transpose(
+                            flipped[:, KB * chunk + 2 * e + wb, :],
+                            lane_max[:, first : first + 2 * P - 1 : 2],
+                            ident_bf[:],
+                        )
             return flipped
 
         def channel_max(b, half, flipped):
             blocks = slice(8 * half, 8 * half + 8)
-            nc.vector.tensor_reduce(out=top[:, b, blocks], in_=flipped[:], axis=AXIS.X, op=ALU.max)
-            nc.vector.tensor_scalar(
-                out=neg_top[:, b, blocks], in0=top[:, b, blocks], scalar1=-1.0, scalar2=None, op0=ALU.mult
+            nc.vector.tensor_reduce(
+                out=neg_top[:, b, blocks], in_=flipped[:], axis=AXIS.X, op=ALU.max, negate=True
             )
 
         def flip(c):
             b, ch = divmod(c, NCH)
+            u_words = u_sb[b][:].bitcast(F32)
             halves = []
-            for half in range(KB // 2):
-                flipped = psum.tile([P, 2, D], BF16, tag="flip", bufs=2)
-                for h in range(2):
-                    tb = KB * ch + 2 * half + h
-                    for j in range(PACK):
-                        nc.tensor.transpose(
-                            flipped[:, h, j * P : (j + 1) * P],
-                            u_sb[b][:, j, tb * TB : (tb + 1) * TB],
-                            ident_bf[:],
-                        )
+            for wb in range(2):
+                first = (2 * ch + wb) * P
+                flipped = psum.tile([P, PACK, P], F32, tag="flip", bufs=2)
+                for j in range(PACK):
+                    nc.tensor.transpose(flipped[:, j, :], u_words[:, j, first : first + P], ident_f32[:])
                 halves.append(flipped)
             return halves
 
         def exponentials(c, halves):
             b, ch = divmod(c, NCH)
             sm_t = work.tile([P, KB, D], F32, tag="sm_t", bufs=2)
-            for k in range(KB):
-                tb = KB * ch + k
-                nc.scalar.activation(
-                    out=sm_t[:, k, :],
-                    in_=halves[k // 2][:, k % 2, :],
-                    func=ACT.Exp,
-                    bias=neg_top[:, b, tb : tb + 1],
-                    scale=1.0,
-                    accum_out=e_sum[:, c, k : k + 1],
-                )
+            for wb in range(2):
+                by_parity = halves[wb][:].bitcast(BF16).rearrange("q j (p e) -> q e j p", e=2)
+                for e in range(2):
+                    k = 2 * e + wb
+                    tb = KB * ch + k
+                    nc.scalar.activation(
+                        out=sm_t[:, k, :].rearrange("q (j p) -> q j p", j=PACK),
+                        in_=by_parity[:, e, :, :],
+                        func=ACT.Exp,
+                        bias=neg_top[:, b, tb : tb + 1],
+                        scale=1.0,
+                        accum_out=e_sum[:, c, k : k + 1],
+                    )
             return sm_t
 
         def invert_sums(c):
@@ -207,10 +211,10 @@ def tile_crosschannelinterp_kernel(tc, x, W_words, W_scales, out):
         def multiply(c, j, sm, a_rows):
             b, ch = divmod(c, NCH)
             nc.vector.scalar_tensor_tensor(
-                out=a_rows[:, j, :],
-                in0=y_sb[b][:, j, ch * CH : (ch + 1) * CH],
+                out=a_rows[:, j, :].rearrange("p (e r) -> p e r", e=2),
+                in0=y_sb[b][:, j, ch * CH : (ch + 1) * CH].rearrange("p (r e) -> p e r", e=2),
                 scalar=mean_by_lane[:, b, j : j + 1],
-                in1=sm[:],
+                in1=sm[:].rearrange("p (e r) -> p e r", e=2),
                 op0=ALU.subtract,
                 op1=ALU.mult,
             )
@@ -250,7 +254,11 @@ def tile_crosschannelinterp_kernel(tc, x, W_words, W_scales, out):
             b, ch = divmod(c, NCH)
             cols = slice(ch * CH, (ch + 1) * CH)
             nc.scalar.activation(
-                out=rep_sb[:, g, :], in_=acc[:], func=ACT.Identity, bias=mean_by_block[:, b, g : g + 1], scale=1.0
+                out=rep_sb[:, g, :].rearrange("p (r e) -> p r e", e=2),
+                in_=acc[:].rearrange("p (e r) -> p r e", e=2),
+                func=ACT.Identity,
+                bias=mean_by_block[:, b, g : g + 1],
+                scale=1.0,
             )
             subtractor = nc.vector if c == NC - 1 else nc.gpsimd
             subtractor.tensor_tensor(
@@ -259,7 +267,9 @@ def tile_crosschannelinterp_kernel(tc, x, W_words, W_scales, out):
             if g % 2 == 1:
                 pair = slice(g - 1, g + 1)
                 nc.sync.dma_start(out=rep_dram[b][:, pair, cols], in_=rep_sb[:, pair, :])
-                nc.sync.dma_start(out=rest_dram[b][:, pair, cols], in_=rest_sb[:, pair, :])
+            if g == G - 1:
+                for pair in (slice(0, 2), slice(2, 4)):
+                    nc.sync.dma_start(out=rest_dram[b][:, pair, cols], in_=rest_sb[:, pair, :])
 
         def intensity(b, j):
             grown = work.tile([P, T], F32, tag="grown", bufs=4)
@@ -295,6 +305,8 @@ def tile_crosschannelinterp_kernel(tc, x, W_words, W_scales, out):
         operands = {}
         for i in range(NC + 1):
             c = i - 1
+            if i + 1 < NC:
+                invert_sums(i + 1)
             if i < NC:
                 a_rows = work.tile([P, PACK, CH], BF16, tag="a_rows")
                 for j in range(PACK):
@@ -317,16 +329,12 @@ def tile_crosschannelinterp_kernel(tc, x, W_words, W_scales, out):
             if i >= 1:
                 for g in (2, 3):
                     finish(c, g, late_sums[g - 2], rep_sb, rest_sb)
-            if i < NC:
-                a_grouped = regroup(a_rows)
             if i + 1 < NC:
-                invert_sums(i + 1)
                 normalise(i + 1, softmaxes[i + 1])
-            if i < NC:
-                operands[i] = quantise(a_grouped)
-            if i + 1 < NC:
                 for j in range(PACK):
                     banks[(i + 1, j)] = back_flip(i + 1, j, softmaxes[i + 1])
+            if i < NC:
+                operands[i] = quantise(regroup(a_rows))
             for b, j in pieces[2 * i + 2 : 2 * i + 4]:
                 intensity(b, j)
             if i in fold_at:

@@ -260,16 +260,18 @@ def tile_crosschannelinterp_kernel(tc, x, W_words, W_scales, out):
                 bias=mean_by_block[:, b, g : g + 1],
                 scale=1.0,
             )
-            subtractor = nc.vector if c == NC - 1 else nc.gpsimd
-            subtractor.tensor_tensor(
-                out=rest_sb[:, g, :], in0=z_sb[b][:, g, cols], in1=rep_sb[:, g, :], op=ALU.subtract
+            nc.vector.scalar_tensor_tensor(
+                out=rest_sb[:, g, :].rearrange("p (r e) -> p r e", e=2),
+                in0=z_sb[b][:, g, cols].rearrange("p (r e) -> p r e", e=2),
+                scalar=mean_by_block[:, b, g : g + 1],
+                in1=acc[:].rearrange("p (e r) -> p r e", e=2),
+                op0=ALU.subtract,
+                op1=ALU.subtract,
             )
             if g % 2 == 1:
                 pair = slice(g - 1, g + 1)
                 nc.sync.dma_start(out=rep_dram[b][:, pair, cols], in_=rep_sb[:, pair, :])
-            if g == G - 1:
-                for pair in (slice(0, 2), slice(2, 4)):
-                    nc.sync.dma_start(out=rest_dram[b][:, pair, cols], in_=rest_sb[:, pair, :])
+                nc.sync.dma_start(out=rest_dram[b][:, pair, cols], in_=rest_sb[:, pair, :])
 
         def intensity(b, j):
             grown = work.tile([P, T], F32, tag="grown", bufs=4)
@@ -315,6 +317,8 @@ def tile_crosschannelinterp_kernel(tc, x, W_words, W_scales, out):
                 channel_max(reduce_at[i][0], reduce_at[i][1], tops[reduce_at[i]])
             if i % NCH == 0 and i < NC:
                 keep_block_means(i // NCH, moved[i // NCH])
+            if i + 1 < NC:
+                normalise(i + 1, softmaxes[i + 1])
             if i >= 1:
                 rep_sb = work.tile([P, G, CH], F32, tag="rep_sb", bufs=3)
                 rest_sb = work.tile([P, G, CH], F32, tag="rest_sb", bufs=3)
@@ -322,19 +326,20 @@ def tile_crosschannelinterp_kernel(tc, x, W_words, W_scales, out):
                     finish(c, g, mix(g, operands[c][0], operands[c][1]), rep_sb, rest_sb)
             if i + 2 < NC:
                 flips[i + 2] = flip(i + 2)
+            if i + 1 < NC:
+                for j in range(PACK):
+                    banks[(i + 1, j)] = back_flip(i + 1, j, softmaxes[i + 1])
             if i >= 1:
                 late_sums = [mix(g, operands[c][0], operands[c][1]) for g in (2, 3)]
             if i + 2 < NC:
                 softmaxes[i + 2] = exponentials(i + 2, flips[i + 2])
+            if i < NC:
+                a_grouped = regroup(a_rows)
             if i >= 1:
                 for g in (2, 3):
                     finish(c, g, late_sums[g - 2], rep_sb, rest_sb)
-            if i + 1 < NC:
-                normalise(i + 1, softmaxes[i + 1])
-                for j in range(PACK):
-                    banks[(i + 1, j)] = back_flip(i + 1, j, softmaxes[i + 1])
             if i < NC:
-                operands[i] = quantise(regroup(a_rows))
+                operands[i] = quantise(a_grouped)
             for b, j in pieces[2 * i + 2 : 2 * i + 4]:
                 intensity(b, j)
             if i in fold_at:

@@ -25,7 +25,7 @@ KB = CH // TB
 NCH = T // CH
 NC = B * NCH
 HALF = T // 2
-AHEAD = 4
+SLOT = (0, 2, 1, 3)
 
 FLOPS = 2 * B * T * D * D
 
@@ -50,8 +50,6 @@ def tile_crosschannelinterp_kernel(tc, x, W_words, W_scales, out):
         z_sb = [inputs.tile([P, G, T], BF16, name="z%d" % b) for b in range(B)]
         w_codes = const.tile([P, PACK * D], U8, align_bytes=64)
         w_scales = const.tile([P, D], U8, align_bytes=64)
-
-        ctx.enter_context(tc.manual_schedule())
 
         nc.vector.memset(w_scales[:].bitcast(I32), 0)
         nc.sync.dma_start(out=u_sb[0][:, :, 0:HALF], in_=u_dram[0][:, :, 0:HALF])
@@ -117,7 +115,7 @@ def tile_crosschannelinterp_kernel(tc, x, W_words, W_scales, out):
                 in1=mean_by_lane[:, b, :].unsqueeze(1).to_broadcast([P, 32, PACK]),
                 op=ALU.mult,
             )
-            moved = psum.tile([P, CH], F32, tag="acc", bufs=2)
+            moved = psum.tile([P, CH], F32, tag="acc")
             nc.tensor.matmul(
                 out=moved[:, 0:G],
                 lhsT=spread[:].rearrange("p r j -> p (r j)"),
@@ -141,16 +139,9 @@ def tile_crosschannelinterp_kernel(tc, x, W_words, W_scales, out):
             return lane_max
 
         def flip_lane_max(lane_max):
-            flipped = psum.tile([P, 8, TB], BF16, tag="flip", bufs=2)
-            for chunk in range(HALF // CH):
-                for e in range(2):
-                    for wb in range(2):
-                        first = chunk * CH + wb * 2 * P + e
-                        nc.tensor.transpose(
-                            flipped[:, KB * chunk + 2 * e + wb, :],
-                            lane_max[:, first : first + 2 * P - 1 : 2],
-                            ident_bf[:],
-                        )
+            flipped = psum.tile([P, HALF // TB, TB], BF16, tag="aw")
+            for k in range(HALF // TB):
+                nc.tensor.transpose(flipped[:, k, :], lane_max[:, k * TB : (k + 1) * TB], ident_bf[:])
             return flipped
 
         def channel_max(b, half, flipped):
@@ -159,73 +150,75 @@ def tile_crosschannelinterp_kernel(tc, x, W_words, W_scales, out):
                 out=neg_top[:, b, blocks], in_=flipped[:], axis=AXIS.X, op=ALU.max, negate=True
             )
 
-        def flip(c):
+        def flip_u(c):
             b, ch = divmod(c, NCH)
-            u_words = u_sb[b][:].bitcast(F32)
-            halves = []
-            for wb in range(2):
-                first = (2 * ch + wb) * P
-                flipped = psum.tile([P, PACK, P], F32, tag="flip", bufs=2)
-                for j in range(PACK):
-                    nc.tensor.transpose(flipped[:, j, :], u_words[:, j, first : first + P], ident_f32[:])
-                halves.append(flipped)
-            return halves
+            pairs = []
+            for half in range(2):
+                u_t = psum.tile([P, 2, PACK, P], BF16, tag="ut")
+                for k in range(2):
+                    first = ch * CH + (2 * half + k) * TB
+                    for j in range(PACK):
+                        nc.tensor.transpose(u_t[:, k, SLOT[j], :], u_sb[b][:, j, first : first + TB], ident_bf[:])
+                pairs.append(u_t)
+            return pairs
 
-        def exponentials(c, halves):
+        def exponential(c, k, pairs, e_t):
             b, ch = divmod(c, NCH)
-            sm_t = work.tile([P, KB, D], F32, tag="sm_t", bufs=2)
-            for wb in range(2):
-                by_parity = halves[wb][:].bitcast(BF16).rearrange("q j (p e) -> q e j p", e=2)
-                for e in range(2):
-                    k = 2 * e + wb
-                    tb = KB * ch + k
-                    nc.scalar.activation(
-                        out=sm_t[:, k, :].rearrange("q (j p) -> q j p", j=PACK),
-                        in_=by_parity[:, e, :, :],
-                        func=ACT.Exp,
-                        bias=neg_top[:, b, tb : tb + 1],
-                        scale=1.0,
-                        accum_out=e_sum[:, c, k : k + 1],
-                    )
-            return sm_t
+            nc.scalar.activation(
+                out=e_t[:, k, :].rearrange("q (w i) -> q w i", i=2),
+                in_=pairs[k // 2][:, k % 2, :, :].rearrange("q (i h) p -> q (h p) i", i=2),
+                func=ACT.Exp,
+                bias=neg_top[:, b, KB * ch + k : KB * ch + k + 1],
+                scale=1.0,
+                accum_out=e_sum[:, c, k : k + 1],
+            )
 
         def invert_sums(c):
             nc.vector.reciprocal(out=e_inv[:, c, :], in_=e_sum[:, c, :])
 
-        def normalise(c, sm_t):
-            for k in range(KB):
-                nc.vector.tensor_scalar(
-                    out=sm_t[:, k, :],
-                    in0=sm_t[:, k, :],
-                    scalar1=e_inv[:, c, k : k + 1],
-                    scalar2=None,
-                    op0=ALU.mult,
-                )
-
-        def back_flip(c, j, sm_t):
-            sm = psum.tile([P, CH], F32, tag="sm", bufs=AHEAD)
-            for k in range(KB):
-                nc.tensor.transpose(sm[:, k * TB : (k + 1) * TB], sm_t[:, k, j * P : (j + 1) * P], ident_f32[:])
-            return sm
-
-        def multiply(c, j, sm, a_rows):
+        def centre(c):
             b, ch = divmod(c, NCH)
+            y_c = work.tile([P, PACK, CH], F32, tag="y_c")
+            for j in range(PACK):
+                nc.vector.tensor_scalar(
+                    out=y_c[:, j, :],
+                    in0=y_sb[b][:, j, ch * CH : (ch + 1) * CH],
+                    scalar1=mean_by_lane[:, b, j : j + 1],
+                    scalar2=None,
+                    op0=ALU.subtract,
+                )
+            return y_c
+
+        def flip_y(k, y_c):
+            y_t = psum.tile([P, PACK, P], F32, tag="yt")
+            for j in range(PACK):
+                nc.tensor.transpose(y_t[:, SLOT[j], :], y_c[:, j, k * TB : (k + 1) * TB], ident_f32[:])
+            return y_t
+
+        def multiply(c, k, e_t, y_t, a_t):
             nc.vector.scalar_tensor_tensor(
-                out=a_rows[:, j, :].rearrange("p (e r) -> p e r", e=2),
-                in0=y_sb[b][:, j, ch * CH : (ch + 1) * CH].rearrange("p (r e) -> p e r", e=2),
-                scalar=mean_by_lane[:, b, j : j + 1],
-                in1=sm[:].rearrange("p (e r) -> p e r", e=2),
-                op0=ALU.subtract,
+                out=a_t[:, k, :].rearrange("q (w i) -> q w i", i=2),
+                in0=e_t[:, k, :].rearrange("q (w i) -> q w i", i=2),
+                scalar=e_inv[:, c, k : k + 1],
+                in1=y_t[:].rearrange("q (i h) p -> q (h p) i", i=2),
+                op0=ALU.mult,
                 op1=ALU.mult,
             )
 
-        def regroup(a_rows):
-            a_grouped = work.tile([P, CH, PACK], BF16, tag="a_grouped", align_bytes=64)
-            nc.vector.tensor_copy(
-                out=a_grouped[:].rearrange("p (c i) j -> p c j i", i=4),
-                in_=a_rows[:].rearrange("p j (c i) -> p c j i", i=4),
+        def flip_a(half, a_t):
+            a_w = psum.tile([P, 2, 2, TB], F32, tag="aw")
+            for k in range(2):
+                words = a_t[:, 2 * half + k, :].bitcast(F32)
+                for h in range(2):
+                    nc.tensor.transpose(a_w[:, k, h, :], words[:, h * P : (h + 1) * P], ident_f32[:])
+            return a_w
+
+        def regroup(half, a_w, a_grouped):
+            words = a_grouped[:].rearrange("p t j -> p (t j)").bitcast(F32)
+            nc.scalar.copy(
+                out=words[:, half * CH : (half + 1) * CH].rearrange("p (k t h) -> p k t h", k=2, h=2),
+                in_=a_w[:].rearrange("p k h t -> p k t h"),
             )
-            return a_grouped
 
         def quantise(a_grouped):
             a_codes = work.tile([P, CH], U32, tag="a_codes", align_bytes=64)
@@ -238,7 +231,7 @@ def tile_crosschannelinterp_kernel(tc, x, W_words, W_scales, out):
             return a_codes, a_scales
 
         def mix(g, a_codes, a_scales):
-            acc = psum.tile([P, CH], F32, tag="acc", bufs=2)
+            acc = psum.tile([P, CH], F32, tag="acc")
             nc.tensor.matmul_mx(
                 out=acc[:],
                 lhsT=w_codes[:, g * PACK * P : (g + 1) * PACK * P].bitcast(FP8X4),
@@ -250,105 +243,132 @@ def tile_crosschannelinterp_kernel(tc, x, W_words, W_scales, out):
             )
             return acc
 
-        def finish(c, g, acc, rep_sb, rest_sb):
-            b, ch = divmod(c, NCH)
-            cols = slice(ch * CH, (ch + 1) * CH)
+        def add_mean(c, g, acc, rep_sb):
+            b = c // NCH
             nc.scalar.activation(
-                out=rep_sb[:, g, :].rearrange("p (r e) -> p r e", e=2),
-                in_=acc[:].rearrange("p (e r) -> p r e", e=2),
-                func=ACT.Identity,
-                bias=mean_by_block[:, b, g : g + 1],
-                scale=1.0,
+                out=rep_sb[:, g, :], in_=acc[:], func=ACT.Identity, bias=mean_by_block[:, b, g : g + 1], scale=1.0
             )
+
+        def subtract(c, g, acc, rest_sb):
+            b, ch = divmod(c, NCH)
             nc.vector.scalar_tensor_tensor(
-                out=rest_sb[:, g, :].rearrange("p (r e) -> p r e", e=2),
-                in0=z_sb[b][:, g, cols].rearrange("p (r e) -> p r e", e=2),
+                out=rest_sb[:, g, :],
+                in0=z_sb[b][:, g, ch * CH : (ch + 1) * CH],
                 scalar=mean_by_block[:, b, g : g + 1],
-                in1=acc[:].rearrange("p (e r) -> p r e", e=2),
+                in1=acc[:],
                 op0=ALU.subtract,
                 op1=ALU.subtract,
             )
-            if g % 2 == 1:
-                pair = slice(g - 1, g + 1)
-                nc.sync.dma_start(out=rep_dram[b][:, pair, cols], in_=rep_sb[:, pair, :])
-                nc.sync.dma_start(out=rest_dram[b][:, pair, cols], in_=rest_sb[:, pair, :])
+
+        def store(c, pair, rep_sb, rest_sb):
+            b, ch = divmod(c, NCH)
+            cols = slice(ch * CH, (ch + 1) * CH)
+            nc.sync.dma_start(out=rep_dram[b][:, pair, cols], in_=rep_sb[:, pair, :])
+            nc.sync.dma_start(out=rest_dram[b][:, pair, cols], in_=rest_sb[:, pair, :])
 
         def intensity(b, j):
-            grown = work.tile([P, T], F32, tag="grown", bufs=4)
+            grown = work.tile([P, T], F32, tag="grown", bufs=3)
             nc.scalar.activation(out=grown[:], in_=u_sb[b][:, j, :], func=ACT.Exp)
             nc.sync.dma_start(out=grown_dram[b][:, j, :], in_=grown[:])
 
-        pieces = [(b, j) for b in range(B) for j in range(PACK)]
-        softmaxes = {}
-        banks = {}
         tops = {}
         moved = {}
+        e_ts = {}
+        y_cs = {}
+        y_ts = {}
+        operands = {}
         tops[(0, 0)] = flip_lane_max(fold_lanes(0, 0))
         time_sum(0, 0)
         channel_max(0, 0, tops[(0, 0)])
-        flips = {0: flip(0)}
-        softmaxes[0] = exponentials(0, flips[0])
+        u_pairs = flip_u(0)
+        e_ts[0] = work.tile([P, KB, D], F32, tag="e_t", name="e_t")
+        for k in range(KB):
+            exponential(0, k, u_pairs, e_ts[0])
         for j in range(1, PACK):
             time_sum(0, j)
         time_mean(0)
+        y_cs[0] = centre(0)
+        for k in (0, 1):
+            y_ts[(0, k)] = flip_y(k, y_cs[0])
         invert_sums(0)
-        normalise(0, softmaxes[0])
-        flips[1] = flip(1)
-        softmaxes[1] = exponentials(1, flips[1])
-        for j in range(PACK):
-            banks[(0, j)] = back_flip(0, j, softmaxes[0])
-        tops[(0, 1)] = flip_lane_max(fold_lanes(0, 1))
         moved[0] = mean_to_blocks(0)
-        intensity(0, 0)
-        intensity(0, 1)
+        keep_block_means(0, moved[0])
 
-        fold_at = {0: (1, 0), 2: (1, 1)}
-        reduce_at = {0: (0, 1), 1: (1, 0), 3: (1, 1)}
-        operands = {}
-        for i in range(NC + 1):
-            c = i - 1
-            if i + 1 < NC:
-                invert_sums(i + 1)
-            if i < NC:
-                a_rows = work.tile([P, PACK, CH], BF16, tag="a_rows")
-                for j in range(PACK):
-                    multiply(i, j, banks[(i, j)], a_rows)
-            if i in reduce_at:
-                channel_max(reduce_at[i][0], reduce_at[i][1], tops[reduce_at[i]])
-            if i % NCH == 0 and i < NC:
-                keep_block_means(i // NCH, moved[i // NCH])
-            if i + 1 < NC:
-                normalise(i + 1, softmaxes[i + 1])
-            if i >= 1:
+        pieces = [(b, j) for b in range(B) for j in range(PACK)]
+        pieces_at = {0: 2, 1: 2, 2: 1, 3: 1, 4: 1, 5: 1}
+        fold_at = {0: (0, 1), 1: (1, 0), 3: (1, 1)}
+        reduce_at = {1: (0, 1), 2: (1, 0), 4: (1, 1)}
+        taken = 0
+        for s in range(NC + 1):
+            nxt, cur, old = s + 1, s, s - 1
+            if s in reduce_at:
+                channel_max(reduce_at[s][0], reduce_at[s][1], tops[reduce_at[s]])
+            if s == NCH:
+                keep_block_means(1, moved[1])
+            sums = {}
+            if old >= 0:
                 rep_sb = work.tile([P, G, CH], F32, tag="rep_sb", bufs=3)
                 rest_sb = work.tile([P, G, CH], F32, tag="rest_sb", bufs=3)
                 for g in (0, 1):
-                    finish(c, g, mix(g, operands[c][0], operands[c][1]), rep_sb, rest_sb)
-            if i + 2 < NC:
-                flips[i + 2] = flip(i + 2)
-            if i + 1 < NC:
-                for j in range(PACK):
-                    banks[(i + 1, j)] = back_flip(i + 1, j, softmaxes[i + 1])
-            if i >= 1:
-                late_sums = [mix(g, operands[c][0], operands[c][1]) for g in (2, 3)]
-            if i + 2 < NC:
-                softmaxes[i + 2] = exponentials(i + 2, flips[i + 2])
-            if i < NC:
-                a_grouped = regroup(a_rows)
-            if i >= 1:
+                    sums[g] = mix(g, operands[old][0], operands[old][1])
+                for g in (0, 1):
+                    add_mean(old, g, sums[g], rep_sb)
+            if cur < NC:
+                a_t = work.tile([P, KB, D], BF16, tag="a_t")
+                a_grouped = work.tile([P, CH, PACK], BF16, tag="a_grouped", align_bytes=64)
+                for k in (0, 1):
+                    multiply(cur, k, e_ts[cur], y_ts[(cur, k)], a_t)
+            if old >= 0:
+                subtract(old, 0, sums[0], rest_sb)
+            if cur < NC:
+                for k in (2, 3):
+                    y_ts[(cur, k)] = flip_y(k, y_cs[cur])
+                a_w = flip_a(0, a_t)
+                regroup(0, a_w, a_grouped)
+            if nxt < NC:
+                u_pairs = flip_u(nxt)
+            if cur < NC:
+                for k in (2, 3):
+                    multiply(cur, k, e_ts[cur], y_ts[(cur, k)], a_t)
+            if old >= 0:
+                subtract(old, 1, sums[1], rest_sb)
+                store(old, slice(0, 2), rep_sb, rest_sb)
+            if nxt < NC:
+                e_ts[nxt] = work.tile([P, KB, D], F32, tag="e_t", name="e_t")
+                for k in (0, 1):
+                    exponential(nxt, k, u_pairs, e_ts[nxt])
+            if cur < NC:
+                a_w = flip_a(1, a_t)
+                regroup(1, a_w, a_grouped)
+            if nxt < NC:
+                for k in (2, 3):
+                    exponential(nxt, k, u_pairs, e_ts[nxt])
+            if old >= 0:
                 for g in (2, 3):
-                    finish(c, g, late_sums[g - 2], rep_sb, rest_sb)
-            if i < NC:
-                operands[i] = quantise(a_grouped)
-            for b, j in pieces[2 * i + 2 : 2 * i + 4]:
+                    sums[g] = mix(g, operands[old][0], operands[old][1])
+            if nxt < NC:
+                y_cs[nxt] = centre(nxt)
+                for k in (0, 1):
+                    y_ts[(nxt, k)] = flip_y(k, y_cs[nxt])
+            if old >= 0:
+                for g in (2, 3):
+                    add_mean(old, g, sums[g], rep_sb)
+                subtract(old, 2, sums[2], rest_sb)
+            if cur < NC:
+                operands[cur] = quantise(a_grouped)
+            if old >= 0:
+                subtract(old, 3, sums[3], rest_sb)
+                store(old, slice(2, 4), rep_sb, rest_sb)
+            if nxt < NC:
+                invert_sums(nxt)
+            for b, j in pieces[taken : taken + pieces_at.get(s, 0)]:
                 intensity(b, j)
-            if i in fold_at:
-                tops[fold_at[i]] = flip_lane_max(fold_lanes(fold_at[i][0], fold_at[i][1]))
-            if i == 1:
-                time_sum(1, 0)
-                time_sum(1, 1)
-            if i == 3:
-                time_sum(1, 2)
-                time_sum(1, 3)
+            taken += pieces_at.get(s, 0)
+            if s in fold_at:
+                tops[fold_at[s]] = flip_lane_max(fold_lanes(fold_at[s][0], fold_at[s][1]))
+            if s == 2:
+                for j in range(PACK):
+                    time_sum(1, j)
                 time_mean(1)
+            if s == 3:
                 moved[1] = mean_to_blocks(1)

@@ -25,6 +25,7 @@ KB = CH // TB
 NCH = T // CH
 NC = B * NCH
 HALF = T // 2
+UNITS = ((0, 0, CH), (0, CH, CH), (0, HALF, HALF), (1, 0, HALF), (1, HALF, HALF))
 SLOT = (0, 2, 1, 3)
 
 FLOPS = 2 * B * T * D * D
@@ -52,9 +53,10 @@ def tile_crosschannelinterp_kernel(tc, x, W_words, W_scales, out):
         w_scales = const.tile([P, D], U8, align_bytes=64)
 
         nc.vector.memset(w_scales[:].bitcast(I32), 0)
-        nc.sync.dma_start(out=u_sb[0][:, :, 0:HALF], in_=u_dram[0][:, :, 0:HALF])
+        nc.sync.dma_start(out=u_sb[0][:, :, 0:CH], in_=u_dram[0][:, :, 0:CH])
         for j in range(PACK):
             nc.sync.dma_start(out=y_sb[0][:, j, :], in_=y_dram[0][:, j, :])
+        nc.sync.dma_start(out=u_sb[0][:, :, CH:HALF], in_=u_dram[0][:, :, CH:HALF])
         nc.sync.dma_start(out=u_sb[0][:, :, HALF:T], in_=u_dram[0][:, :, HALF:T])
         nc.sync.dma_start(
             out=w_codes[:].bitcast(I32),
@@ -102,6 +104,22 @@ def tile_crosschannelinterp_kernel(tc, x, W_words, W_scales, out):
                 accum_out=y_sum[:, b, j : j + 1],
             )
 
+        def time_sum_on_scalar(b, j):
+            scrap_s = work.tile([P, T], BF16, tag="grown", bufs=3)
+            nc.scalar.activation(out=scrap_s[:], in_=y_sb[b][:, j, :], func=ACT.Copy, accum_out=y_sum[:, b, j : j + 1])
+
+        def time_sum_by_matmul(b, j):
+            folded_y = psum.tile([P, CH], F32, tag="aw")
+            for k in range(T // P):
+                nc.tensor.matmul(
+                    out=folded_y[:, 0:P],
+                    lhsT=ident_bf[:],
+                    rhs=y_sb[b][:, j, k * P : (k + 1) * P],
+                    start=(k == 0),
+                    stop=(k == T // P - 1),
+                )
+            nc.vector.tensor_reduce(out=y_sum[:, b, j : j + 1], in_=folded_y[:, 0:P], axis=AXIS.X, op=ALU.add)
+
         def time_mean(b):
             nc.vector.tensor_scalar(
                 out=mean_by_lane[:, b, :], in0=y_sum[:, b, :], scalar1=1.0 / T, scalar2=None, op0=ALU.mult
@@ -128,45 +146,54 @@ def tile_crosschannelinterp_kernel(tc, x, W_words, W_scales, out):
         def keep_block_means(b, moved):
             nc.vector.tensor_copy(out=mean_by_block[:, b, :], in_=moved[:, 0:G])
 
-        def fold_lanes(b, half):
-            cols = slice(half * HALF, (half + 1) * HALF)
-            pair_a = work.tile([P, HALF], BF16, tag="pair_a", bufs=1)
+        def fold_lanes(b, first, width):
+            cols = slice(first, first + width)
+            pair_a = work.tile([P, width], BF16, tag="pair_a", bufs=1)
             nc.vector.tensor_tensor(out=pair_a[:], in0=u_sb[b][:, 0, cols], in1=u_sb[b][:, 1, cols], op=ALU.max)
-            pair_b = work.tile([P, HALF], BF16, tag="pair_b", bufs=1)
+            pair_b = work.tile([P, width], BF16, tag="pair_b", bufs=1)
             nc.vector.tensor_tensor(out=pair_b[:], in0=u_sb[b][:, 2, cols], in1=u_sb[b][:, 3, cols], op=ALU.max)
-            lane_max = work.tile([P, HALF], BF16, tag="lane_max", bufs=1)
+            lane_max = work.tile([P, width], BF16, tag="lane_max", bufs=1)
             nc.vector.tensor_tensor(out=lane_max[:], in0=pair_a[:], in1=pair_b[:], op=ALU.max)
             return lane_max
 
-        def flip_lane_max(lane_max):
-            flipped = psum.tile([P, HALF // TB, TB], BF16, tag="aw")
-            for k in range(HALF // TB):
-                nc.tensor.transpose(flipped[:, k, :], lane_max[:, k * TB : (k + 1) * TB], ident_bf[:])
+        def flip_lane_max(lane_max, width):
+            flipped = psum.tile([P, width // (2 * TB), TB], F32, tag="aw")
+            words = lane_max[:].bitcast(F32)
+            for w in range(width // (2 * TB)):
+                nc.tensor.transpose(flipped[:, w, :], words[:, w * TB : (w + 1) * TB], ident_f32[:])
             return flipped
 
-        def channel_max(b, half, flipped):
-            blocks = slice(8 * half, 8 * half + 8)
+        def channel_max(b, first, width, flipped):
+            blocks = slice(first // TB, (first + width) // TB)
             nc.vector.tensor_reduce(
-                out=neg_top[:, b, blocks], in_=flipped[:], axis=AXIS.X, op=ALU.max, negate=True
+                out=neg_top[:, b, blocks].rearrange("q (w e) -> q w e", e=2),
+                in_=flipped[:].bitcast(BF16).rearrange("q w (p e) -> q w e p", e=2),
+                axis=AXIS.X,
+                op=ALU.max,
+                negate=True,
             )
+
+        def start_maxima(unit):
+            return flip_lane_max(fold_lanes(unit[0], unit[1], unit[2]), unit[2])
 
         def flip_u(c):
             b, ch = divmod(c, NCH)
+            words = u_sb[b][:].bitcast(F32)
             pairs = []
-            for half in range(2):
-                u_t = psum.tile([P, 2, PACK, P], BF16, tag="ut")
-                for k in range(2):
-                    first = ch * CH + (2 * half + k) * TB
-                    for j in range(PACK):
-                        nc.tensor.transpose(u_t[:, k, SLOT[j], :], u_sb[b][:, j, first : first + TB], ident_bf[:])
+            for w in range(2):
+                u_t = psum.tile([P, PACK, P], F32, tag="ut")
+                first = (2 * ch + w) * P
+                for j in range(PACK):
+                    nc.tensor.transpose(u_t[:, SLOT[j], :], words[:, j, first : first + P], ident_f32[:])
                 pairs.append(u_t)
             return pairs
 
         def exponential(c, k, pairs, e_t):
             b, ch = divmod(c, NCH)
+            by_parity = pairs[k // 2][:].bitcast(BF16).rearrange("q (i h) (p e) -> q e (h p) i", i=2, e=2)
             nc.scalar.activation(
                 out=e_t[:, k, :].rearrange("q (w i) -> q w i", i=2),
-                in_=pairs[k // 2][:, k % 2, :, :].rearrange("q (i h) p -> q (h p) i", i=2),
+                in_=by_parity[:, k % 2, :, :],
                 func=ACT.Exp,
                 bias=neg_top[:, b, KB * ch + k : KB * ch + k + 1],
                 scale=1.0,
@@ -181,8 +208,8 @@ def tile_crosschannelinterp_kernel(tc, x, W_words, W_scales, out):
             y_c = work.tile([P, PACK, CH], F32, tag="y_c")
             for j in range(PACK):
                 nc.vector.tensor_scalar(
-                    out=y_c[:, j, :],
-                    in0=y_sb[b][:, j, ch * CH : (ch + 1) * CH],
+                    out=y_c[:, j, :].rearrange("p (e r) -> p e r", e=2),
+                    in0=y_sb[b][:, j, ch * CH : (ch + 1) * CH].rearrange("p (r e) -> p e r", e=2),
                     scalar1=mean_by_lane[:, b, j : j + 1],
                     scalar2=None,
                     op0=ALU.subtract,
@@ -191,8 +218,9 @@ def tile_crosschannelinterp_kernel(tc, x, W_words, W_scales, out):
 
         def flip_y(k, y_c):
             y_t = psum.tile([P, PACK, P], F32, tag="yt")
+            first = (k % 2) * (CH // 2) + (k // 2) * TB
             for j in range(PACK):
-                nc.tensor.transpose(y_t[:, SLOT[j], :], y_c[:, j, k * TB : (k + 1) * TB], ident_f32[:])
+                nc.tensor.transpose(y_t[:, SLOT[j], :], y_c[:, j, first : first + TB], ident_f32[:])
             return y_t
 
         def multiply(c, k, e_t, y_t, a_t):
@@ -216,8 +244,8 @@ def tile_crosschannelinterp_kernel(tc, x, W_words, W_scales, out):
         def regroup(half, a_w, a_grouped):
             words = a_grouped[:].rearrange("p t j -> p (t j)").bitcast(F32)
             nc.scalar.copy(
-                out=words[:, half * CH : (half + 1) * CH].rearrange("p (k t h) -> p k t h", k=2, h=2),
-                in_=a_w[:].rearrange("p k h t -> p k t h"),
+                out=words[:, half * CH : (half + 1) * CH].rearrange("p (q e h) -> p q e h", e=2, h=2),
+                in_=a_w[:].rearrange("p e h q -> p q e h"),
             )
 
         def quantise(a_grouped):
@@ -230,8 +258,8 @@ def tile_crosschannelinterp_kernel(tc, x, W_words, W_scales, out):
             )
             return a_codes, a_scales
 
-        def mix(g, a_codes, a_scales):
-            acc = psum.tile([P, CH], F32, tag="acc")
+        def mix(g, a_codes, a_scales, tag="acc"):
+            acc = psum.tile([P, CH], F32, tag=tag)
             nc.tensor.matmul_mx(
                 out=acc[:],
                 lhsT=w_codes[:, g * PACK * P : (g + 1) * PACK * P].bitcast(FP8X4),
@@ -277,32 +305,35 @@ def tile_crosschannelinterp_kernel(tc, x, W_words, W_scales, out):
         y_cs = {}
         y_ts = {}
         operands = {}
-        tops[(0, 0)] = flip_lane_max(fold_lanes(0, 0))
-        time_sum(0, 0)
-        channel_max(0, 0, tops[(0, 0)])
+        tops[0] = start_maxima(UNITS[0])
+        time_sum_on_scalar(0, 0)
+        time_sum_on_scalar(0, 1)
+        channel_max(UNITS[0][0], UNITS[0][1], UNITS[0][2], tops[0])
         u_pairs = flip_u(0)
         e_ts[0] = work.tile([P, KB, D], F32, tag="e_t", name="e_t")
         for k in range(KB):
             exponential(0, k, u_pairs, e_ts[0])
-        for j in range(1, PACK):
+        for j in range(2, PACK):
             time_sum(0, j)
         time_mean(0)
         y_cs[0] = centre(0)
         for k in (0, 1):
             y_ts[(0, k)] = flip_y(k, y_cs[0])
         invert_sums(0)
+        tops[1] = start_maxima(UNITS[1])
         moved[0] = mean_to_blocks(0)
         keep_block_means(0, moved[0])
 
         pieces = [(b, j) for b in range(B) for j in range(PACK)]
         pieces_at = {0: 2, 1: 2, 2: 1, 3: 1, 4: 1, 5: 1}
-        fold_at = {0: (0, 1), 1: (1, 0), 3: (1, 1)}
-        reduce_at = {1: (0, 1), 2: (1, 0), 4: (1, 1)}
+        fold_at = {0: 2, 1: 3, 3: 4}
+        reduce_at = {0: 1, 1: 2, 2: 3, 4: 4}
         taken = 0
-        for s in range(NC + 1):
+        for s in range(NC):
             nxt, cur, old = s + 1, s, s - 1
             if s in reduce_at:
-                channel_max(reduce_at[s][0], reduce_at[s][1], tops[reduce_at[s]])
+                unit = UNITS[reduce_at[s]]
+                channel_max(unit[0], unit[1], unit[2], tops[reduce_at[s]])
             if s == NCH:
                 keep_block_means(1, moved[1])
             sums = {}
@@ -365,10 +396,27 @@ def tile_crosschannelinterp_kernel(tc, x, W_words, W_scales, out):
                 intensity(b, j)
             taken += pieces_at.get(s, 0)
             if s in fold_at:
-                tops[fold_at[s]] = flip_lane_max(fold_lanes(fold_at[s][0], fold_at[s][1]))
+                tops[fold_at[s]] = start_maxima(UNITS[fold_at[s]])
+            if s == 1:
+                time_sum_by_matmul(1, 0)
             if s == 2:
-                for j in range(PACK):
-                    time_sum(1, j)
+                time_sum_by_matmul(1, 1)
+                time_sum_by_matmul(1, 2)
+                time_sum(1, 3)
                 time_mean(1)
             if s == 3:
                 moved[1] = mean_to_blocks(1)
+
+        old = NC - 1
+        b, ch = divmod(old, NCH)
+        cols = slice(ch * CH, (ch + 1) * CH)
+        rep_sb = work.tile([P, G, CH], F32, tag="rep_sb", bufs=3)
+        rest_sb = work.tile([P, G, CH], F32, tag="rest_sb", bufs=3)
+        sums = [mix(g, operands[old][0], operands[old][1], tag) for g, tag in enumerate(("acc", "acc", "yt", "yt"))]
+        for turn in range(G):
+            g_s, g_v = turn, (turn + 2) % G
+            add_mean(old, g_s, sums[g_s], rep_sb)
+            subtract(old, g_v, sums[g_v], rest_sb)
+            if turn % 2 == 1:
+                nc.sync.dma_start(out=rep_dram[b][:, g_s - 1 : g_s + 1, cols], in_=rep_sb[:, g_s - 1 : g_s + 1, :])
+                nc.sync.dma_start(out=rest_dram[b][:, g_v - 1 : g_v + 1, cols], in_=rest_sb[:, g_v - 1 : g_v + 1, :])

@@ -26,6 +26,8 @@ NCH = T // CH
 NC = B * NCH
 HALF = T // 2
 UNITS = ((0, 0, CH), (0, CH, CH), (0, HALF, HALF), (1, 0, HALF), (1, HALF, HALF))
+VECTOR_ADDS = (0, 1, 2, 3)
+Z1_STEP = 1
 SLOT = (0, 2, 1, 3)
 
 FLOPS = 2 * B * T * D * D
@@ -70,7 +72,6 @@ def tile_crosschannelinterp_kernel(tc, x, W_words, W_scales, out):
         nc.sync.dma_start(out=z_sb[0][:], in_=z_dram[0])
         nc.sync.dma_start(out=u_sb[1][:], in_=u_dram[1])
         nc.sync.dma_start(out=y_sb[1][:], in_=y_dram[1])
-        nc.sync.dma_start(out=z_sb[1][:], in_=z_dram[1])
 
         ident_bf = const.tile([P, P], BF16)
         make_identity(nc, ident_bf[:])
@@ -120,9 +121,9 @@ def tile_crosschannelinterp_kernel(tc, x, W_words, W_scales, out):
                 )
             nc.vector.tensor_reduce(out=y_sum[:, b, j : j + 1], in_=folded_y[:, 0:P], axis=AXIS.X, op=ALU.add)
 
-        def time_mean(b):
+        def time_mean(b, lanes):
             nc.vector.tensor_scalar(
-                out=mean_by_lane[:, b, :], in0=y_sum[:, b, :], scalar1=1.0 / T, scalar2=None, op0=ALU.mult
+                out=mean_by_lane[:, b, lanes], in0=y_sum[:, b, lanes], scalar1=1.0 / T, scalar2=None, op0=ALU.mult
             )
 
         def mean_to_blocks(b):
@@ -273,9 +274,14 @@ def tile_crosschannelinterp_kernel(tc, x, W_words, W_scales, out):
 
         def add_mean(c, g, acc, rep_sb):
             b = c // NCH
-            nc.scalar.activation(
-                out=rep_sb[:, g, :], in_=acc[:], func=ACT.Identity, bias=mean_by_block[:, b, g : g + 1], scale=1.0
-            )
+            if g == G - 1 and c in VECTOR_ADDS:
+                nc.vector.tensor_scalar(
+                    out=rep_sb[:, g, :], in0=acc[:], scalar1=mean_by_block[:, b, g : g + 1], scalar2=None, op0=ALU.add
+                )
+            else:
+                nc.scalar.activation(
+                    out=rep_sb[:, g, :], in_=acc[:], func=ACT.Identity, bias=mean_by_block[:, b, g : g + 1], scale=1.0
+                )
 
         def subtract(c, g, acc, rest_sb):
             b, ch = divmod(c, NCH)
@@ -313,9 +319,10 @@ def tile_crosschannelinterp_kernel(tc, x, W_words, W_scales, out):
         e_ts[0] = work.tile([P, KB, D], F32, tag="e_t", name="e_t")
         for k in range(KB):
             exponential(0, k, u_pairs, e_ts[0])
-        for j in range(2, PACK):
-            time_sum(0, j)
-        time_mean(0)
+        time_sum(0, 2)
+        time_mean(0, slice(0, 3))
+        time_sum(0, 3)
+        time_mean(0, slice(3, 4))
         y_cs[0] = centre(0)
         for k in (0, 1):
             y_ts[(0, k)] = flip_y(k, y_cs[0])
@@ -331,6 +338,8 @@ def tile_crosschannelinterp_kernel(tc, x, W_words, W_scales, out):
         taken = 0
         for s in range(NC):
             nxt, cur, old = s + 1, s, s - 1
+            if s == Z1_STEP:
+                nc.sync.dma_start(out=z_sb[1][:], in_=z_dram[1])
             if s in reduce_at:
                 unit = UNITS[reduce_at[s]]
                 channel_max(unit[0], unit[1], unit[2], tops[reduce_at[s]])
@@ -403,7 +412,7 @@ def tile_crosschannelinterp_kernel(tc, x, W_words, W_scales, out):
                 time_sum_by_matmul(1, 1)
                 time_sum_by_matmul(1, 2)
                 time_sum(1, 3)
-                time_mean(1)
+                time_mean(1, slice(0, PACK))
             if s == 3:
                 moved[1] = mean_to_blocks(1)
 
@@ -417,6 +426,5 @@ def tile_crosschannelinterp_kernel(tc, x, W_words, W_scales, out):
             g_s, g_v = turn, (turn + 2) % G
             add_mean(old, g_s, sums[g_s], rep_sb)
             subtract(old, g_v, sums[g_v], rest_sb)
-            if turn % 2 == 1:
-                nc.sync.dma_start(out=rep_dram[b][:, g_s - 1 : g_s + 1, cols], in_=rep_sb[:, g_s - 1 : g_s + 1, :])
-                nc.sync.dma_start(out=rest_dram[b][:, g_v - 1 : g_v + 1, cols], in_=rest_sb[:, g_v - 1 : g_v + 1, :])
+            nc.sync.dma_start(out=rep_dram[b][:, g_s, cols], in_=rep_sb[:, g_s, :])
+            nc.sync.dma_start(out=rest_dram[b][:, g_v, cols], in_=rest_sb[:, g_v, :])

@@ -27,7 +27,7 @@ NC = B * NCH
 HALF = T // 2
 UNITS = ((0, 0, CH), (0, CH, CH), (0, HALF, HALF), (1, 0, HALF), (1, HALF, HALF))
 VECTOR_ADDS = (0, 1, 2, 3)
-Z1_STEP = 1
+Z1_STEP = 3
 SLOT = (0, 2, 1, 3)
 
 FLOPS = 2 * B * T * D * D
@@ -50,7 +50,7 @@ def tile_crosschannelinterp_kernel(tc, x, W_words, W_scales, out):
 
         y_sb = [inputs.tile([P, PACK, T], BF16, name="y%d" % b) for b in range(B)]
         u_sb = [inputs.tile([P, PACK, T], BF16, name="u%d" % b) for b in range(B)]
-        z_sb = [inputs.tile([P, G, T], BF16, name="z%d" % b) for b in range(B)]
+        z_sb = [inputs.tile([P, G, T], BF16, name="z0")]
         w_codes = const.tile([P, PACK * D], U8, align_bytes=64)
         w_scales = const.tile([P, D], U8, align_bytes=64)
 
@@ -339,6 +339,7 @@ def tile_crosschannelinterp_kernel(tc, x, W_words, W_scales, out):
         for s in range(NC):
             nxt, cur, old = s + 1, s, s - 1
             if s == Z1_STEP:
+                z_sb.append(inputs.tile([P, G, T], BF16, name="y0"))
                 nc.sync.dma_start(out=z_sb[1][:], in_=z_dram[1])
             if s in reduce_at:
                 unit = UNITS[reduce_at[s]]
@@ -347,8 +348,8 @@ def tile_crosschannelinterp_kernel(tc, x, W_words, W_scales, out):
                 keep_block_means(1, moved[1])
             sums = {}
             if old >= 0:
-                rep_sb = work.tile([P, G, CH], F32, tag="rep_sb", bufs=3)
-                rest_sb = work.tile([P, G, CH], F32, tag="rest_sb", bufs=3)
+                rep_sb = work.tile([P, G, CH], F32, tag="rep_sb", bufs=4)
+                rest_sb = work.tile([P, G, CH], F32, tag="rest_sb", bufs=4)
                 for g in (0, 1):
                     sums[g] = mix(g, operands[old][0], operands[old][1])
                 for g in (0, 1):
@@ -419,8 +420,8 @@ def tile_crosschannelinterp_kernel(tc, x, W_words, W_scales, out):
         old = NC - 1
         b, ch = divmod(old, NCH)
         cols = slice(ch * CH, (ch + 1) * CH)
-        rep_sb = work.tile([P, G, CH], F32, tag="rep_sb", bufs=3)
-        rest_sb = work.tile([P, G, CH], F32, tag="rest_sb", bufs=3)
+        rep_sb = work.tile([P, G, CH], F32, tag="rep_sb", bufs=4)
+        rest_sb = work.tile([P, G, CH], F32, tag="rest_sb", bufs=4)
         sums = [mix(g, operands[old][0], operands[old][1], tag) for g, tag in enumerate(("acc", "acc", "yt", "yt"))]
         for turn in range(G):
             g_s, g_v = turn, (turn + 2) % G

@@ -49,17 +49,24 @@ def tile_crosschannelinterp_kernel(tc, x, W_words, W_scales, out):
         rest_dram = [out[b, 2 * D : 3 * D, :].rearrange("(g m) t -> m g t", m=P) for b in range(B)]
 
         y_sb = [inputs.tile([P, PACK, T], BF16, name="y%d" % b) for b in range(B)]
-        u_sb = [inputs.tile([P, PACK, T], BF16, name="u%d" % b) for b in range(B)]
+        u0_sb = inputs.tile([P, NCH, PACK, CH], BF16, name="u0")
+        u1_sb = inputs.tile([P, PACK, T], BF16, name="u1")
+
+        def u_lane(b, j, first, width):
+            if b == 0:
+                return u0_sb[:, first // CH : (first + width) // CH, j, :]
+            return u1_sb[:, j, first : first + width].rearrange("p (c t) -> p c t", t=CH)
+
         z_sb = [inputs.tile([P, G, T], BF16, name="z0")]
         w_codes = const.tile([P, PACK * D], U8, align_bytes=64)
         w_scales = const.tile([P, D], U8, align_bytes=64)
 
         nc.vector.memset(w_scales[:].bitcast(I32), 0)
-        nc.sync.dma_start(out=u_sb[0][:, :, 0:CH], in_=u_dram[0][:, :, 0:CH])
+        nc.sync.dma_start(out=u0_sb[:, 0, :, :], in_=u_dram[0][:, :, 0:CH])
         for j in range(PACK):
             nc.sync.dma_start(out=y_sb[0][:, j, :], in_=y_dram[0][:, j, :])
-        nc.sync.dma_start(out=u_sb[0][:, :, CH:HALF], in_=u_dram[0][:, :, CH:HALF])
-        nc.sync.dma_start(out=u_sb[0][:, :, HALF:T], in_=u_dram[0][:, :, HALF:T])
+        for ch in range(1, NCH):
+            nc.sync.dma_start(out=u0_sb[:, ch, :, :], in_=u_dram[0][:, :, ch * CH : (ch + 1) * CH])
         nc.sync.dma_start(
             out=w_codes[:].bitcast(I32),
             in_=W_words[0].rearrange("p n t -> p (n t)").bitcast(I32),
@@ -70,7 +77,7 @@ def tile_crosschannelinterp_kernel(tc, x, W_words, W_scales, out):
                 in_=W_scales[0, 4 * q : 4 * q + 4, :].bitcast(I32),
             )
         nc.sync.dma_start(out=z_sb[0][:], in_=z_dram[0])
-        nc.sync.dma_start(out=u_sb[1][:], in_=u_dram[1])
+        nc.sync.dma_start(out=u1_sb[:], in_=u_dram[1])
         nc.sync.dma_start(out=y_sb[1][:], in_=y_dram[1])
 
         ident_bf = const.tile([P, P], BF16)
@@ -148,11 +155,20 @@ def tile_crosschannelinterp_kernel(tc, x, W_words, W_scales, out):
             nc.vector.tensor_copy(out=mean_by_block[:, b, :], in_=moved[:, 0:G])
 
         def fold_lanes(b, first, width):
-            cols = slice(first, first + width)
             pair_a = work.tile([P, width], BF16, tag="pair_a", bufs=1)
-            nc.vector.tensor_tensor(out=pair_a[:], in0=u_sb[b][:, 0, cols], in1=u_sb[b][:, 1, cols], op=ALU.max)
+            nc.vector.tensor_tensor(
+                out=pair_a[:].rearrange("p (c t) -> p c t", t=CH),
+                in0=u_lane(b, 0, first, width),
+                in1=u_lane(b, 1, first, width),
+                op=ALU.max,
+            )
             pair_b = work.tile([P, width], BF16, tag="pair_b", bufs=1)
-            nc.vector.tensor_tensor(out=pair_b[:], in0=u_sb[b][:, 2, cols], in1=u_sb[b][:, 3, cols], op=ALU.max)
+            nc.vector.tensor_tensor(
+                out=pair_b[:].rearrange("p (c t) -> p c t", t=CH),
+                in0=u_lane(b, 2, first, width),
+                in1=u_lane(b, 3, first, width),
+                op=ALU.max,
+            )
             lane_max = work.tile([P, width], BF16, tag="lane_max", bufs=1)
             nc.vector.tensor_tensor(out=lane_max[:], in0=pair_a[:], in1=pair_b[:], op=ALU.max)
             return lane_max
@@ -179,13 +195,15 @@ def tile_crosschannelinterp_kernel(tc, x, W_words, W_scales, out):
 
         def flip_u(c):
             b, ch = divmod(c, NCH)
-            words = u_sb[b][:].bitcast(F32)
             pairs = []
             for w in range(2):
                 u_t = psum.tile([P, PACK, P], F32, tag="ut")
-                first = (2 * ch + w) * P
                 for j in range(PACK):
-                    nc.tensor.transpose(u_t[:, SLOT[j], :], words[:, j, first : first + P], ident_f32[:])
+                    if b == 0:
+                        words = u0_sb[:, ch, j, w * 2 * P : (w + 1) * 2 * P].bitcast(F32)
+                    else:
+                        words = u1_sb[:, j, ch * CH + w * 2 * P : ch * CH + (w + 1) * 2 * P].bitcast(F32)
+                    nc.tensor.transpose(u_t[:, SLOT[j], :], words, ident_f32[:])
                 pairs.append(u_t)
             return pairs
 
@@ -302,7 +320,7 @@ def tile_crosschannelinterp_kernel(tc, x, W_words, W_scales, out):
 
         def intensity(b, j):
             grown = work.tile([P, T], F32, tag="grown", bufs=3)
-            nc.scalar.activation(out=grown[:], in_=u_sb[b][:, j, :], func=ACT.Exp)
+            nc.scalar.activation(out=grown[:].rearrange("p (c t) -> p c t", t=CH), in_=u_lane(b, j, 0, T), func=ACT.Exp)
             nc.sync.dma_start(out=grown_dram[b][:, j, :], in_=grown[:])
 
         tops = {}
@@ -311,25 +329,26 @@ def tile_crosschannelinterp_kernel(tc, x, W_words, W_scales, out):
         y_cs = {}
         y_ts = {}
         operands = {}
-        tops[0] = start_maxima(UNITS[0])
-        time_sum_on_scalar(0, 0)
-        time_sum_on_scalar(0, 1)
-        channel_max(UNITS[0][0], UNITS[0][1], UNITS[0][2], tops[0])
-        u_pairs = flip_u(0)
-        e_ts[0] = work.tile([P, KB, D], F32, tag="e_t", name="e_t")
-        for k in range(KB):
-            exponential(0, k, u_pairs, e_ts[0])
-        time_sum(0, 2)
-        time_mean(0, slice(0, 3))
-        time_sum(0, 3)
-        time_mean(0, slice(3, 4))
-        y_cs[0] = centre(0)
-        for k in (0, 1):
-            y_ts[(0, k)] = flip_y(k, y_cs[0])
-        invert_sums(0)
-        tops[1] = start_maxima(UNITS[1])
-        moved[0] = mean_to_blocks(0)
-        keep_block_means(0, moved[0])
+        with tc.manual_schedule(engines={mybir.EngineType.PE, mybir.EngineType.DVE}):
+            tops[0] = start_maxima(UNITS[0])
+            time_sum_on_scalar(0, 0)
+            time_sum_on_scalar(0, 1)
+            channel_max(UNITS[0][0], UNITS[0][1], UNITS[0][2], tops[0])
+            u_pairs = flip_u(0)
+            e_ts[0] = work.tile([P, KB, D], F32, tag="e_t", name="e_t")
+            for k in range(KB):
+                exponential(0, k, u_pairs, e_ts[0])
+            time_sum(0, 2)
+            time_mean(0, slice(0, 3))
+            time_sum(0, 3)
+            time_mean(0, slice(3, 4))
+            y_cs[0] = centre(0)
+            for k in (0, 1):
+                y_ts[(0, k)] = flip_y(k, y_cs[0])
+            invert_sums(0)
+            tops[1] = start_maxima(UNITS[1])
+            moved[0] = mean_to_blocks(0)
+            keep_block_means(0, moved[0])
 
         pieces = [(b, j) for b in range(B) for j in range(PACK)]
         pieces_at = {0: 2, 1: 2, 2: 1, 3: 1, 4: 1, 5: 1}

@@ -301,6 +301,15 @@ def tile_crosschannelinterp_kernel(tc, x, W_words, W_scales, out):
                     out=rep_sb[:, g, :], in_=acc[:], func=ACT.Identity, bias=mean_by_block[:, b, g : g + 1], scale=1.0
                 )
 
+        def subtract_rep(c, pair, rep_sb, rest_sb):
+            b, ch = divmod(c, NCH)
+            nc.vector.tensor_tensor(
+                out=rest_sb[:, pair, :],
+                in0=z_sb[b][:, pair, ch * CH : (ch + 1) * CH],
+                in1=rep_sb[:, pair, :],
+                op=ALU.subtract,
+            )
+
         def subtract(c, g, acc, rest_sb):
             b, ch = divmod(c, NCH)
             nc.vector.scalar_tensor_tensor(
@@ -378,8 +387,6 @@ def tile_crosschannelinterp_kernel(tc, x, W_words, W_scales, out):
                 a_grouped = work.tile([P, CH, PACK], BF16, tag="a_grouped", align_bytes=64)
                 for k in (0, 1):
                     multiply(cur, k, e_ts[cur], y_ts[(cur, k)], a_t)
-            if old >= 0:
-                subtract(old, 0, sums[0], rest_sb)
             if cur < NC:
                 for k in (2, 3):
                     y_ts[(cur, k)] = flip_y(k, y_cs[cur])
@@ -391,7 +398,7 @@ def tile_crosschannelinterp_kernel(tc, x, W_words, W_scales, out):
                 for k in (2, 3):
                     multiply(cur, k, e_ts[cur], y_ts[(cur, k)], a_t)
             if old >= 0:
-                subtract(old, 1, sums[1], rest_sb)
+                subtract_rep(old, slice(0, 2), rep_sb, rest_sb)
                 store(old, slice(0, 2), rep_sb, rest_sb)
             if nxt < NC:
                 e_ts[nxt] = work.tile([P, KB, D], F32, tag="e_t", name="e_t")
@@ -413,11 +420,10 @@ def tile_crosschannelinterp_kernel(tc, x, W_words, W_scales, out):
             if old >= 0:
                 for g in (2, 3):
                     add_mean(old, g, sums[g], rep_sb)
-                subtract(old, 2, sums[2], rest_sb)
             if cur < NC:
                 operands[cur] = quantise(a_grouped)
             if old >= 0:
-                subtract(old, 3, sums[3], rest_sb)
+                subtract_rep(old, slice(2, 4), rep_sb, rest_sb)
                 store(old, slice(2, 4), rep_sb, rest_sb)
             if nxt < NC:
                 invert_sums(nxt)

@@ -1,7 +1,6 @@
 from contextlib import ExitStack
 
 import concourse.mybir as mybir
-from concourse.masks import make_identity
 
 F32 = mybir.dt.float32
 BF16 = mybir.dt.bfloat16
@@ -80,14 +79,23 @@ def tile_crosschannelinterp_kernel(tc, x, W_words, W_scales, out):
         nc.sync.dma_start(out=u1_sb[:], in_=u_dram[1])
         nc.sync.dma_start(out=y_sb[1][:], in_=y_dram[1])
 
-        ident_bf = const.tile([P, P], BF16)
-        make_identity(nc, ident_bf[:])
-        ident_f32 = const.tile([P, P], F32)
-        make_identity(nc, ident_f32[:])
-        lane_mask = const.tile([P, 32], F32)
-        nc.vector.tensor_reduce(
-            out=lane_mask[:], in_=ident_f32[:].rearrange("p (q r) -> p r q", q=4), axis=AXIS.X, op=ALU.add
+        ones = const.tile([P, 32], F32)
+        nc.vector.memset(ones[:], 1.0)
+        counts = const.tile([P, 32], F32, align_bytes=64)
+        nc.vector.tensor_tensor_scan(
+            out=counts[:], data0=ones[:], data1=ones[:], initial=0.0, op0=ALU.mult, op1=ALU.add
         )
+        turned = const.tile([P, 32], F32, align_bytes=64)
+        nc.vector.transpose(turned[:], counts[:])
+        lane_mask = const.tile([P, 32], F32)
+        nc.vector.tensor_tensor(out=lane_mask[:], in0=counts[:], in1=turned[:], op=ALU.is_equal)
+        ident_f32 = const.tile([P, P], F32)
+        nc.vector.memset(ident_f32[:], 0.0)
+        for q in range(4):
+            block = slice(32 * q, 32 * q + 32)
+            nc.vector.tensor_copy(out=ident_f32[block, block], in_=lane_mask[block, :])
+        ident_bf = const.tile([P, P], BF16)
+        nc.vector.tensor_copy(out=ident_bf[:], in_=ident_f32[:])
         quad_mask = const.tile([P, G], F32)
         nc.vector.tensor_reduce(
             out=quad_mask[:], in_=ident_f32[:].rearrange("p (g r) -> p g r", g=G), axis=AXIS.X, op=ALU.add

from contextlib import ExitStack

import concourse.mybir as mybir

F32 = mybir.dt.float32
BF16 = mybir.dt.bfloat16
I32 = mybir.dt.int32
U32 = mybir.dt.uint32
U8 = mybir.dt.uint8
FP8X4 = mybir.dt.float8_e4m3fn_x4
ALU = mybir.AluOpType
ACT = mybir.ActivationFunctionType
AXIS = mybir.AxisListType

B = 2
D = 512
T = 2048
P = 128
PACK = 4
G = D // P
TB = P
CH = 512
KB = CH // TB
NCH = T // CH
NC = B * NCH
HALF = T // 2
UNITS = ((0, 0, CH), (0, CH, CH), (0, HALF, HALF), (1, 0, HALF), (1, HALF, HALF))
VECTOR_ADDS = (0, 1, 2, 3)
Z1_STEP = 3
SLOT = (0, 2, 1, 3)

FLOPS = 2 * B * T * D * D


def tile_crosschannelinterp_kernel(tc, x, W_words, W_scales, out):
    nc = tc.nc
    with ExitStack() as ctx:
        const = ctx.enter_context(tc.tile_pool(name="const", bufs=1))
        inputs = ctx.enter_context(tc.tile_pool(name="inputs", bufs=1))
        work = ctx.enter_context(tc.tile_pool(name="work", bufs=2))
        psum = ctx.enter_context(tc.psum_pool(name="psum", bufs=2))

        y_dram = [x[b, 0:D, :].rearrange("(p j) t -> p j t", j=PACK) for b in range(B)]
        u_dram = [x[b, D : 2 * D, :].rearrange("(p j) t -> p j t", j=PACK) for b in range(B)]
        z_dram = [x[b, 2 * D : 3 * D, :].rearrange("(g m) t -> m g t", m=P) for b in range(B)]
        rep_dram = [out[b, 0:D, :].rearrange("(g m) t -> m g t", m=P) for b in range(B)]
        grown_dram = [out[b, D : 2 * D, :].rearrange("(p j) t -> p j t", j=PACK) for b in range(B)]
        rest_dram = [out[b, 2 * D : 3 * D, :].rearrange("(g m) t -> m g t", m=P) for b in range(B)]

        y_sb = [inputs.tile([P, PACK, T], BF16, name="y%d" % b) for b in range(B)]
        u0_sb = inputs.tile([P, NCH, PACK, CH], BF16, name="u0")
        u1_sb = inputs.tile([P, PACK, T], BF16, name="u1")

        def u_lane(b, j, first, width):
            if b == 0:
                return u0_sb[:, first // CH : (first + width) // CH, j, :]
            return u1_sb[:, j, first : first + width].rearrange("p (c t) -> p c t", t=CH)

        z_sb = [inputs.tile([P, G, T], BF16, name="z0")]
        w_codes = const.tile([P, PACK * D], U8, align_bytes=64)
        w_scales = const.tile([P, D], U8, align_bytes=64)

        nc.vector.memset(w_scales[:].bitcast(I32), 0)
        nc.sync.dma_start(out=u0_sb[:, 0, :, :], in_=u_dram[0][:, :, 0:CH])
        for j in range(PACK):
            nc.sync.dma_start(out=y_sb[0][:, j, :], in_=y_dram[0][:, j, :])
        for ch in range(1, NCH):
            nc.sync.dma_start(out=u0_sb[:, ch, :, :], in_=u_dram[0][:, :, ch * CH : (ch + 1) * CH])
        nc.sync.dma_start(
            out=w_codes[:].bitcast(I32),
            in_=W_words[0].rearrange("p n t -> p (n t)").bitcast(I32),
        )
        for q in range(4):
            nc.sync.dma_start(
                out=w_scales[32 * q : 32 * q + 4, :].bitcast(I32),
                in_=W_scales[0, 4 * q : 4 * q + 4, :].bitcast(I32),
            )
        nc.sync.dma_start(out=z_sb[0][:], in_=z_dram[0])
        nc.sync.dma_start(out=u1_sb[:], in_=u_dram[1])
        nc.sync.dma_start(out=y_sb[1][:], in_=y_dram[1])

        ones = const.tile([P, 32], F32)
        nc.vector.memset(ones[:], 1.0)
        counts = const.tile([P, 32], F32, align_bytes=64)
        nc.vector.tensor_tensor_scan(
            out=counts[:], data0=ones[:], data1=ones[:], initial=0.0, op0=ALU.mult, op1=ALU.add
        )
        turned = const.tile([P, 32], F32, align_bytes=64)
        nc.vector.transpose(turned[:], counts[:])
        lane_mask = const.tile([P, 32], F32)
        nc.vector.tensor_tensor(out=lane_mask[:], in0=counts[:], in1=turned[:], op=ALU.is_equal)
        ident_f32 = const.tile([P, P], F32)
        nc.vector.memset(ident_f32[:], 0.0)
        for q in range(4):
            block = slice(32 * q, 32 * q + 32)
            nc.vector.tensor_copy(out=ident_f32[block, block], in_=lane_mask[block, :])
        ident_bf = const.tile([P, P], BF16)
        nc.vector.tensor_copy(out=ident_bf[:], in_=ident_f32[:])
        quad_mask = const.tile([P, G], F32)
        nc.vector.tensor_reduce(
            out=quad_mask[:], in_=ident_f32[:].rearrange("p (g r) -> p g r", g=G), axis=AXIS.X, op=ALU.add
        )

        y_sum = const.tile([P, B, PACK], F32)
        mean_by_lane = const.tile([P, B, PACK], F32)
        mean_by_block = const.tile([P, B, G], F32)
        neg_top = const.tile([P, B, T // TB], F32)
        e_sum = const.tile([P, NC, KB], F32)
        e_inv = const.tile([P, NC, KB], F32)

        def time_sum(b, j):
            scrap = work.tile([P, T], BF16, tag="scrap", bufs=1)
            nc.vector.tensor_scalar(
                out=scrap[:],
                in0=y_sb[b][:, j, :],
                scalar1=1.0,
                scalar2=None,
                op0=ALU.mult,
                op1=ALU.add,
                accum_out=y_sum[:, b, j : j + 1],
            )

        def time_sum_on_scalar(b, j):
            scrap_s = work.tile([P, T], BF16, tag="grown", bufs=3)
            nc.scalar.activation(out=scrap_s[:], in_=y_sb[b][:, j, :], func=ACT.Copy, accum_out=y_sum[:, b, j : j + 1])

        def time_sum_by_matmul(b, j):
            folded_y = psum.tile([P, CH], F32, tag="aw")
            for k in range(T // P):
                nc.tensor.matmul(
                    out=folded_y[:, 0:P],
                    lhsT=ident_bf[:],
                    rhs=y_sb[b][:, j, k * P : (k + 1) * P],
                    start=(k == 0),
                    stop=(k == T // P - 1),
                )
            nc.vector.tensor_reduce(out=y_sum[:, b, j : j + 1], in_=folded_y[:, 0:P], axis=AXIS.X, op=ALU.add)

        def time_mean(b, lanes):
            nc.vector.tensor_scalar(
                out=mean_by_lane[:, b, lanes], in0=y_sum[:, b, lanes], scalar1=1.0 / T, scalar2=None, op0=ALU.mult
            )

        def mean_to_blocks(b):
            spread = work.tile([P, 32, PACK], F32, tag="spread")
            nc.vector.tensor_tensor(
                out=spread[:],
                in0=lane_mask[:].unsqueeze(2).to_broadcast([P, 32, PACK]),
                in1=mean_by_lane[:, b, :].unsqueeze(1).to_broadcast([P, 32, PACK]),
                op=ALU.mult,
            )
            moved = psum.tile([P, CH], F32, tag="acc")
            nc.tensor.matmul(
                out=moved[:, 0:G],
                lhsT=spread[:].rearrange("p r j -> p (r j)"),
                rhs=quad_mask[:],
                start=True,
                stop=True,
            )
            return moved

        def keep_block_means(b, moved):
            nc.vector.tensor_copy(out=mean_by_block[:, b, :], in_=moved[:, 0:G])

        def fold_lanes(b, first, width):
            pair_a = work.tile([P, width], BF16, tag="pair_a", bufs=1)
            nc.vector.tensor_tensor(
                out=pair_a[:].rearrange("p (c t) -> p c t", t=CH),
                in0=u_lane(b, 0, first, width),
                in1=u_lane(b, 1, first, width),
                op=ALU.max,
            )
            pair_b = work.tile([P, width], BF16, tag="pair_b", bufs=1)
            nc.vector.tensor_tensor(
                out=pair_b[:].rearrange("p (c t) -> p c t", t=CH),
                in0=u_lane(b, 2, first, width),
                in1=u_lane(b, 3, first, width),
                op=ALU.max,
            )
            lane_max = work.tile([P, width], BF16, tag="lane_max", bufs=1)
            nc.vector.tensor_tensor(out=lane_max[:], in0=pair_a[:], in1=pair_b[:], op=ALU.max)
            return lane_max

        def flip_lane_max(lane_max, width):
            flipped = psum.tile([P, width // (2 * TB), TB], F32, tag="aw")
            words = lane_max[:].bitcast(F32)
            for w in range(width // (2 * TB)):
                nc.tensor.transpose(flipped[:, w, :], words[:, w * TB : (w + 1) * TB], ident_f32[:])
            return flipped

        def channel_max(b, first, width, flipped):
            blocks = slice(first // TB, (first + width) // TB)
            nc.vector.tensor_reduce(
                out=neg_top[:, b, blocks].rearrange("q (w e) -> q w e", e=2),
                in_=flipped[:].bitcast(BF16).rearrange("q w (p e) -> q w e p", e=2),
                axis=AXIS.X,
                op=ALU.max,
                negate=True,
            )

        def start_maxima(unit):
            return flip_lane_max(fold_lanes(unit[0], unit[1], unit[2]), unit[2])

        def flip_u(c):
            b, ch = divmod(c, NCH)
            pairs = []
            for w in range(2):
                u_t = psum.tile([P, PACK, P], F32, tag="ut")
                for j in range(PACK):
                    if b == 0:
                        words = u0_sb[:, ch, j, w * 2 * P : (w + 1) * 2 * P].bitcast(F32)
                    else:
                        words = u1_sb[:, j, ch * CH + w * 2 * P : ch * CH + (w + 1) * 2 * P].bitcast(F32)
                    nc.tensor.transpose(u_t[:, SLOT[j], :], words, ident_f32[:])
                pairs.append(u_t)
            return pairs

        def exponential(c, k, pairs, e_t):
            b, ch = divmod(c, NCH)
            by_parity = pairs[k // 2][:].bitcast(BF16).rearrange("q (i h) (p e) -> q e (h p) i", i=2, e=2)
            nc.scalar.activation(
                out=e_t[:, k, :].rearrange("q (w i) -> q w i", i=2),
                in_=by_parity[:, k % 2, :, :],
                func=ACT.Exp,
                bias=neg_top[:, b, KB * ch + k : KB * ch + k + 1],
                scale=1.0,
                accum_out=e_sum[:, c, k : k + 1],
            )

        def invert_sums(c):
            nc.vector.reciprocal(out=e_inv[:, c, :], in_=e_sum[:, c, :])

        def centre(c):
            b, ch = divmod(c, NCH)
            y_c = work.tile([P, PACK, CH], F32, tag="y_c")
            for j in range(PACK):
                nc.vector.tensor_scalar(
                    out=y_c[:, j, :].rearrange("p (e r) -> p e r", e=2),
                    in0=y_sb[b][:, j, ch * CH : (ch + 1) * CH].rearrange("p (r e) -> p e r", e=2),
                    scalar1=mean_by_lane[:, b, j : j + 1],
                    scalar2=None,
                    op0=ALU.subtract,
                )
            return y_c

        def flip_y(k, y_c):
            y_t = psum.tile([P, PACK, P], F32, tag="yt")
            first = (k % 2) * (CH // 2) + (k // 2) * TB
            for j in range(PACK):
                nc.tensor.transpose(y_t[:, SLOT[j], :], y_c[:, j, first : first + TB], ident_f32[:])
            return y_t

        def multiply(c, k, e_t, y_t, a_t):
            nc.vector.scalar_tensor_tensor(
                out=a_t[:, k, :].rearrange("q (w i) -> q w i", i=2),
                in0=e_t[:, k, :].rearrange("q (w i) -> q w i", i=2),
                scalar=e_inv[:, c, k : k + 1],
                in1=y_t[:].rearrange("q (i h) p -> q (h p) i", i=2),
                op0=ALU.mult,
                op1=ALU.mult,
            )

        def flip_a(half, a_t):
            a_w = psum.tile([P, 2, 2, TB], F32, tag="aw")
            for k in range(2):
                words = a_t[:, 2 * half + k, :].bitcast(F32)
                for h in range(2):
                    nc.tensor.transpose(a_w[:, k, h, :], words[:, h * P : (h + 1) * P], ident_f32[:])
            return a_w

        def regroup(half, a_w, a_grouped):
            words = a_grouped[:].rearrange("p t j -> p (t j)").bitcast(F32)
            nc.scalar.copy(
                out=words[:, half * CH : (half + 1) * CH].rearrange("p (q e h) -> p q e h", e=2, h=2),
                in_=a_w[:].rearrange("p e h q -> p q e h"),
            )

        def quantise(a_grouped):
            a_codes = work.tile([P, CH], U32, tag="a_codes", align_bytes=64)
            a_scales = work.tile([P, CH], U8, tag="a_scales", align_bytes=64)
            nc.vector.quantize_mx(
                out=a_codes[:].bitcast(FP8X4),
                scales=a_scales[:],
                in_=a_grouped[:].rearrange("p t j -> p (t j)"),
            )
            return a_codes, a_scales

        def mix(g, a_codes, a_scales, tag="acc"):
            acc = psum.tile([P, CH], F32, tag=tag)
            nc.tensor.matmul_mx(
                out=acc[:],
                lhsT=w_codes[:, g * PACK * P : (g + 1) * PACK * P].bitcast(FP8X4),
                lhsT_scale=w_scales[:, g * P : (g + 1) * P],
                rhs=a_codes[:].bitcast(FP8X4),
                rhs_scale=a_scales[:],
                start=True,
                stop=True,
            )
            return acc

        def add_mean(c, g, acc, rep_sb):
            b = c // NCH
            if g == G - 1 and c in VECTOR_ADDS:
                nc.vector.tensor_scalar(
                    out=rep_sb[:, g, :], in0=acc[:], scalar1=mean_by_block[:, b, g : g + 1], scalar2=None, op0=ALU.add
                )
            else:
                nc.scalar.activation(
                    out=rep_sb[:, g, :], in_=acc[:], func=ACT.Identity, bias=mean_by_block[:, b, g : g + 1], scale=1.0
                )

        def subtract_rep(c, pair, rep_sb, rest_sb):
            b, ch = divmod(c, NCH)
            nc.vector.tensor_tensor(
                out=rest_sb[:, pair, :],
                in0=z_sb[b][:, pair, ch * CH : (ch + 1) * CH],
                in1=rep_sb[:, pair, :],
                op=ALU.subtract,
            )

        def subtract(c, g, acc, rest_sb):
            b, ch = divmod(c, NCH)
            nc.vector.scalar_tensor_tensor(
                out=rest_sb[:, g, :],
                in0=z_sb[b][:, g, ch * CH : (ch + 1) * CH],
                scalar=mean_by_block[:, b, g : g + 1],
                in1=acc[:],
                op0=ALU.subtract,
                op1=ALU.subtract,
            )

        def store(c, pair, rep_sb, rest_sb):
            b, ch = divmod(c, NCH)
            cols = slice(ch * CH, (ch + 1) * CH)
            nc.sync.dma_start(out=rep_dram[b][:, pair, cols], in_=rep_sb[:, pair, :])
            nc.sync.dma_start(out=rest_dram[b][:, pair, cols], in_=rest_sb[:, pair, :])

        def intensity(b, j):
            grown = work.tile([P, T], F32, tag="grown", bufs=3)
            nc.scalar.activation(out=grown[:].rearrange("p (c t) -> p c t", t=CH), in_=u_lane(b, j, 0, T), func=ACT.Exp)
            nc.sync.dma_start(out=grown_dram[b][:, j, :], in_=grown[:])

        tops = {}
        moved = {}
        e_ts = {}
        y_cs = {}
        y_ts = {}
        operands = {}
        with tc.manual_schedule(engines={mybir.EngineType.PE, mybir.EngineType.DVE}):
            tops[0] = start_maxima(UNITS[0])
            time_sum_on_scalar(0, 0)
            time_sum_on_scalar(0, 1)
            channel_max(UNITS[0][0], UNITS[0][1], UNITS[0][2], tops[0])
            u_pairs = flip_u(0)
            e_ts[0] = work.tile([P, KB, D], F32, tag="e_t", name="e_t")
            for k in range(KB):
                exponential(0, k, u_pairs, e_ts[0])
            time_sum(0, 2)
            time_mean(0, slice(0, 3))
            time_sum(0, 3)
            time_mean(0, slice(3, 4))
            y_cs[0] = centre(0)
            for k in (0, 1):
                y_ts[(0, k)] = flip_y(k, y_cs[0])
            invert_sums(0)
            tops[1] = start_maxima(UNITS[1])
            moved[0] = mean_to_blocks(0)
            keep_block_means(0, moved[0])

        pieces = [(b, j) for b in range(B) for j in range(PACK)]
        pieces_at = {0: 2, 1: 2, 2: 1, 3: 1, 4: 1, 5: 1}
        fold_at = {0: 2, 1: 3, 3: 4}
        reduce_at = {0: 1, 1: 2, 2: 3, 4: 4}
        taken = 0
        for s in range(NC):
            nxt, cur, old = s + 1, s, s - 1
            if s == Z1_STEP:
                z_sb.append(inputs.tile([P, G, T], BF16, name="y0"))
                nc.sync.dma_start(out=z_sb[1][:], in_=z_dram[1])
            if s in reduce_at:
                unit = UNITS[reduce_at[s]]
                channel_max(unit[0], unit[1], unit[2], tops[reduce_at[s]])
            if s == NCH:
                keep_block_means(1, moved[1])
            sums = {}
            if old >= 0:
                rep_sb = work.tile([P, G, CH], F32, tag="rep_sb", bufs=4)
                rest_sb = work.tile([P, G, CH], F32, tag="rest_sb", bufs=4)
                for g in (0, 1):
                    sums[g] = mix(g, operands[old][0], operands[old][1])
                for g in (0, 1):
                    add_mean(old, g, sums[g], rep_sb)
            if cur < NC:
                a_t = work.tile([P, KB, D], BF16, tag="a_t")
                a_grouped = work.tile([P, CH, PACK], BF16, tag="a_grouped", align_bytes=64)
                for k in (0, 1):
                    multiply(cur, k, e_ts[cur], y_ts[(cur, k)], a_t)
            if cur < NC:
                for k in (2, 3):
                    y_ts[(cur, k)] = flip_y(k, y_cs[cur])
                a_w = flip_a(0, a_t)
                regroup(0, a_w, a_grouped)
            if nxt < NC:
                u_pairs = flip_u(nxt)
            if cur < NC:
                for k in (2, 3):
                    multiply(cur, k, e_ts[cur], y_ts[(cur, k)], a_t)
            if old >= 0:
                subtract_rep(old, slice(0, 2), rep_sb, rest_sb)
                store(old, slice(0, 2), rep_sb, rest_sb)
            if nxt < NC:
                e_ts[nxt] = work.tile([P, KB, D], F32, tag="e_t", name="e_t")
                for k in (0, 1):
                    exponential(nxt, k, u_pairs, e_ts[nxt])
            if cur < NC:
                a_w = flip_a(1, a_t)
                regroup(1, a_w, a_grouped)
            if nxt < NC:
                for k in (2, 3):
                    exponential(nxt, k, u_pairs, e_ts[nxt])
            if old >= 0:
                for g in (2, 3):
                    sums[g] = mix(g, operands[old][0], operands[old][1])
            if nxt < NC:
                y_cs[nxt] = centre(nxt)
                for k in (0, 1):
                    y_ts[(nxt, k)] = flip_y(k, y_cs[nxt])
            if old >= 0:
                for g in (2, 3):
                    add_mean(old, g, sums[g], rep_sb)
            if cur < NC:
                operands[cur] = quantise(a_grouped)
            if old >= 0:
                subtract_rep(old, slice(2, 4), rep_sb, rest_sb)
                store(old, slice(2, 4), rep_sb, rest_sb)
            if nxt < NC:
                invert_sums(nxt)
            for b, j in pieces[taken : taken + pieces_at.get(s, 0)]:
                intensity(b, j)
            taken += pieces_at.get(s, 0)
            if s in fold_at:
                tops[fold_at[s]] = start_maxima(UNITS[fold_at[s]])
            if s == 1:
                time_sum_by_matmul(1, 0)
            if s == 2:
                time_sum_by_matmul(1, 1)
                time_sum_by_matmul(1, 2)
                time_sum(1, 3)
                time_mean(1, slice(0, PACK))
            if s == 3:
                moved[1] = mean_to_blocks(1)

        old = NC - 1
        b, ch = divmod(old, NCH)
        cols = slice(ch * CH, (ch + 1) * CH)
        rep_sb = work.tile([P, G, CH], F32, tag="rep_sb", bufs=4)
        rest_sb = work.tile([P, G, CH], F32, tag="rest_sb", bufs=4)
        sums = [mix(g, operands[old][0], operands[old][1], tag) for g, tag in enumerate(("acc", "acc", "yt", "yt"))]
        for turn in range(G):
            g_s, g_v = turn, (turn + 2) % G
            add_mean(old, g_s, sums[g_s], rep_sb)
            subtract(old, g_v, sums[g_v], rest_sb)
            nc.sync.dma_start(out=rep_dram[b][:, g_s, cols], in_=rep_sb[:, g_s, :])
            nc.sync.dma_start(out=rest_dram[b][:, g_v, cols], in_=rest_sb[:, g_v, :])
